import numpy as np
import ml_dtypes


def mxq(x, axis, fmt="e4m3"):
    dtype, down = {"e4m3": (ml_dtypes.float8_e4m3fn, 7), "e5m2": (ml_dtypes.float8_e5m2, 14)}[fmt]
    v = np.moveaxis(np.asarray(x, np.float32).astype(ml_dtypes.bfloat16).astype(np.float64), axis, -1)
    blocks = v.reshape(v.shape[:-1] + (-1, 32))
    amax = np.abs(blocks).max(-1, keepdims=True)
    byte = np.maximum(np.where(amax > 0, np.frexp(amax)[1] - 1 + 127, 0) - down, 1)
    scale = np.exp2(byte - 127.0)
    codes = (blocks / scale).astype(np.float32).astype(dtype).astype(np.float64)
    return np.moveaxis((codes * scale).reshape(v.shape), -1, axis)


WIDE = False


def mx_kscale(k):
    if not WIDE:
        return np.ones(k)
    levels = np.array([10, -10, 5, -5, 0])
    a = np.random.permutation(np.resize(levels, k // 512 * 4)).reshape(k // 512, 4)
    idx = np.arange(k)
    return np.exp2(a[idx // 512, idx % 128 // 32])


BF16 = ml_dtypes.bfloat16


def bf(x):
    return np.asarray(x, np.float32).astype(BF16)


def f64(x):
    return np.asarray(x).astype(np.float64)


E2M1 = np.array([0.0, 0.5, 1.0, 1.5, 2.0, 3.0, 4.0, 6.0, -0.0, -0.5, -1.0, -1.5, -2.0, -3.0, -4.0, -6.0])


def pack_weight(w, fmt):
    k, n = w.shape
    w = f64(bf(w)).reshape(k // 32, 32, n)
    amax = np.abs(w).max(1)
    if fmt == "e4m3":
        byte = np.frexp(amax)[1] - 1 + 127 - 7
    else:
        mant, ex = np.frexp(amax / 6.0)
        byte = np.where(mant > 0.5, ex, ex - 1) + 127
    byte = np.clip(np.where(amax > 0, byte, 1), 1, 254)
    scaled = (w * np.exp2(127.0 - byte)[:, None, :]).reshape(k, n).astype(np.float32)
    by_word = np.ascontiguousarray(scaled.reshape(k // 512, 128, 4, n).transpose(0, 1, 3, 2))
    if fmt == "e4m3":
        words = by_word.astype(ml_dtypes.float8_e4m3fn).view(np.uint8)
    else:
        c = by_word.astype(ml_dtypes.float4_e2m1fn).view(np.uint8) & 0xF
        words = c[..., 0::2] | (c[..., 1::2] << 4)
    return np.ascontiguousarray(words), np.ascontiguousarray(byte.astype(np.uint8).reshape(k // 512, 16, n))


def unpack_weight(words, scales, fmt):
    g, p, n, _ = words.shape
    if fmt == "e4m3":
        vals = np.ascontiguousarray(words).view(ml_dtypes.float8_e4m3fn).astype(np.float64)
    else:
        nib = np.empty((g, p, n, 4), np.uint8)
        nib[..., 0::2] = words & 0xF
        nib[..., 1::2] = words >> 4
        vals = E2M1[nib]
    vals = vals * np.repeat(np.exp2(scales.astype(np.float64) - 127.0), 8, axis=1)[..., None]
    return vals.transpose(0, 1, 3, 2).reshape(g * 512, n)


B, Nx, Nh, Ny, G = 2048, 2048, 512, 1024, 4
NU = 1.0


def setup_inputs():
    s = mx_kscale(Nx)
    base = np.random.standard_normal((G, Nx))
    w = np.random.standard_normal((Nh, Nx)) * np.sqrt(24.0 / (Nx * Nh))
    b = np.random.standard_normal(Nh) * 2.0 / np.sqrt(Nh)
    hid = np.stack([np.maximum((w * np.maximum(base[g], 0.0)).sum(axis=1) + b, 0.0) for g in range(G)])
    x = np.sqrt(0.75) * base[np.random.randint(0, G, B)] + 0.5 * np.random.standard_normal((B, Nx))
    wq = np.random.uniform(0.5, 1.5, (Ny, 1)) * hid[np.random.randint(0, G, Ny)] + np.random.standard_normal((Ny, Nh)) / np.sqrt(Nh)
    words, scales = pack_weight((w / s[None, :]).T, "e4m3")
    return {"x": bf(x * s),
            "W_fc_words": words,
            "W_fc_scales": scales,
            "b_fc": bf(b),
            "W_q": bf(wq)}


def reference(x, W_fc_words, W_fc_scales, b_fc, W_q):
    wq = f64(W_q)
    a = np.maximum(f64(x), 0.0)
    h = np.maximum((mxq(a, 1, "e4m3") @ unpack_weight(W_fc_words, W_fc_scales, "e4m3")) + f64(b_fc), 0.0)
    d = (np.sum(h * h, axis=-1, keepdims=True)
         - 2.0 * (mxq(h, 1, "e4m3") @ mxq(wq, 1, "e4m3").T)
         + np.sum(wq * wq, axis=-1))
    d = np.maximum(d, 0.0)
    t = (-(NU + 1.0) / 2.0) * np.log1p(d / NU)
    m = t.max(axis=-1, keepdims=True)
    return t - (m + np.log(np.sum(np.exp(t - m), axis=-1, keepdims=True)))

@@ -1,0 +1,307 @@
+from contextlib import ExitStack
+
+import concourse.mybir as mybir
+from concourse.masks import make_identity
+
+F32 = mybir.dt.float32
+BF16 = mybir.dt.bfloat16
+I32 = mybir.dt.int32
+U32 = mybir.dt.uint32
+U8 = mybir.dt.uint8
+FP8X4 = mybir.dt.float8_e4m3fn_x4
+ACT = mybir.ActivationFunctionType
+ALU = mybir.AluOpType
+
+P = 128
+B, NX, NH, NY = 2048, 2048, 512, 1024
+K_PASS = 4 * P
+N_PASS = NX // K_PASS
+N_HID = NH // P
+CHUNK = 512
+ROW_TILES = CHUNK // P
+N_CHUNK = B // CHUNK
+N_HALF = NY // 512
+HID_ON_SCALAR = 2
+LAG_HIDDEN, LAG_DIST, LAG_LOGS, LAG_FINISH = 4, 8, 12, 17
+
+FLOPS = 2 * B * NX * NH + 2 * B * NH * NY
+
+
+def tile_tnet_kernel(tc, x, W_fc_words, W_fc_scales, b_fc, W_q, out):
+    nc = tc.nc
+    with ExitStack() as ctx:
+        keep = ctx.enter_context(tc.tile_pool(name="keep", bufs=1))
+        work = ctx.enter_context(tc.tile_pool(name="work", bufs=2))
+        psum = ctx.enter_context(tc.psum_pool(name="psum", bufs=1))
+        ctx.enter_context(tc.manual_schedule())
+
+        x_tiles = []
+
+        def load_x(rt):
+            x_rt = work.tile([P, NX], BF16, tag="x_rt", bufs=8)
+            nc.sync.dma_start(out=x_rt[:], in_=x[rt * P : (rt + 1) * P, :])
+            x_tiles.append(x_rt)
+
+        wq_rows = keep.tile([P, NY // P, NH], BF16)
+        nc.sync.dma_start(out=wq_rows[:], in_=W_q.rearrange("(a p) k -> p a k", p=P))
+        for rt in range(ROW_TILES):
+            load_x(rt)
+
+        w_planes = keep.tile([P, N_PASS, NH], U8, align_bytes=64)
+        nc.vector.memset(w_planes[:].bitcast(I32), 0)
+        for quad in range(4):
+            nc.sync.dma_start(
+                out=w_planes[32 * quad : 32 * quad + 4, :, :].bitcast(I32),
+                in_=W_fc_scales[:, 4 * quad : 4 * quad + 4, :].rearrange("g r n -> r g n").bitcast(I32),
+            )
+        w_codes = keep.tile([P, N_PASS, NH], U32, align_bytes=64)
+        nc.sync.dma_start(
+            out=w_codes[:].bitcast(I32),
+            in_=W_fc_words.rearrange("g p n t -> p g (n t)").bitcast(I32),
+        )
+        bias_rows = keep.tile([P, P], BF16)
+        nc.vector.memset(bias_rows[:], 0.0)
+        nc.sync.dma_start(out=bias_rows[0:N_HID, :], in_=b_fc.rearrange("(c p) -> c p", p=P))
+        for rt in range(ROW_TILES, B // P):
+            load_x(rt)
+
+        ident_f32 = keep.tile([P, P], F32)
+        make_identity(nc, ident_f32[:])
+        ident_bf16 = keep.tile([P, P], BF16)
+        make_identity(nc, ident_bf16[:])
+        ones = keep.tile([P, 2], F32)
+        nc.vector.memset(ones[:], 1.0)
+
+        bias = keep.tile([P, N_HID], F32)
+
+        def spread_bias():
+            bias_ps = psum.tile([P, P], BF16, tag="hh")
+            nc.tensor.transpose(bias_ps[:], bias_rows[:], ident_bf16[:])
+            nc.vector.tensor_copy(out=bias[:], in_=bias_ps[:, 0:N_HID])
+
+        ww_col = keep.tile([P, NY // P], F32)
+        wq_grouped = keep.tile([P, NY, 4], BF16, align_bytes=64)
+        for pair in range(NY // P // 2):
+            wq_ps = psum.tile([P, 2, 4, P], BF16, tag="xt", bufs=3)
+            for a in range(2):
+                for t in range(4):
+                    nc.tensor.transpose(
+                        wq_ps[:, a, t, :], wq_rows[:, 2 * pair + a, t * P : (t + 1) * P], ident_bf16[:]
+                    )
+            nc.vector.tensor_copy(
+                out=wq_grouped[:, 2 * pair * P : (2 * pair + 2) * P, :].rearrange("p (a j) t -> p a j t", a=2),
+                in_=wq_ps[:].rearrange("p a t j -> p a j t"),
+            )
+        for a in range(NY // P):
+            squares = work.tile([P, NH], F32, tag="squares")
+            nc.scalar.activation(
+                out=squares[:], in_=wq_rows[:, a, :], func=ACT.Square, accum_out=ww_col[:, a : a + 1]
+            )
+        wq_codes = keep.tile([P, NY], U32, align_bytes=64)
+        wq_scales = keep.tile([P, NY], U8, align_bytes=64)
+        nc.vector.quantize_mx(
+            out=wq_codes[:].bitcast(FP8X4),
+            scales=wq_scales[:],
+            in_=wq_grouped[:].rearrange("p j t -> p (j t)"),
+        )
+        ww_half = keep.tile([P, NY], F32)
+        for half in range(N_HALF):
+            ww_ps = psum.tile([P, 512], F32, tag="acc2", bufs=2)
+            for a in range(4):
+                nc.tensor.matmul(
+                    out=ww_ps[:, a * P : (a + 1) * P],
+                    lhsT=ww_col[:, 4 * half + a : 4 * half + a + 1].to_broadcast([P, P]),
+                    rhs=ident_f32[:],
+                    start=True,
+                    stop=True,
+                )
+            nc.scalar.mul(out=ww_half[:, 512 * half : 512 * (half + 1)], in_=ww_ps[:], mul=0.5)
+
+        state = {}
+
+        def relu(chunk, r):
+            x_rt = x_tiles[chunk * ROW_TILES + r]
+            nc.vector.tensor_scalar_max(out=x_rt[:], in0=x_rt[:], scalar1=0.0)
+
+        def transpose_row_tile(chunk, r):
+            if r == 0:
+                a_grouped = work.tile([P, N_PASS, CHUNK, 4], BF16, tag="a_grouped", align_bytes=64)
+                state["a_grouped", chunk] = a_grouped
+            a_words = state["a_grouped", chunk][:].bitcast(F32)
+            x_words = x_tiles[chunk * ROW_TILES + r][:].bitcast(F32)
+            for pair in range(N_PASS // 2):
+                xt = psum.tile([P, 2, 2, P], F32, tag="xt", bufs=3)
+                for gi in range(2):
+                    g = 2 * pair + gi
+                    for u in range(2):
+                        nc.tensor.transpose(
+                            xt[:, gi, u, :], x_words[:, 256 * g + u : 256 * (g + 1) : 2], ident_f32[:]
+                        )
+                nc.scalar.copy(
+                    out=a_words[:, 2 * pair : 2 * pair + 2, r * P : (r + 1) * P, :],
+                    in_=xt[:].rearrange("p g u i -> p g i u"),
+                )
+
+        def quantise_a(chunk):
+            a_codes = work.tile([P, N_PASS, CHUNK], U32, tag="a_codes", align_bytes=64)
+            a_scales = work.tile([P, N_PASS, CHUNK], U8, tag="a_scales", align_bytes=64)
+            for g in range(N_PASS):
+                nc.vector.quantize_mx(
+                    out=a_codes[:, g, :].bitcast(FP8X4),
+                    scales=a_scales[:, g, :],
+                    in_=state["a_grouped", chunk][:, g, :, :].rearrange("p b t -> p (b t)"),
+                )
+            state["a", chunk] = (a_codes, a_scales)
+
+        def hidden_chunk(chunk, c):
+            if c == 0:
+                h_f32 = work.tile([P, N_HID, CHUNK], F32, tag="h_f32")
+                h_sq = work.tile([P, N_HID, CHUNK], F32, tag="h_sq")
+                state["h", chunk] = (h_f32, h_sq)
+            h_f32, h_sq = state["h", chunk]
+            a_codes, a_scales = state["a", chunk]
+            acc1 = psum.tile([P, CHUNK], F32, tag="acc1", bufs=2)
+            for g in range(N_PASS):
+                nc.tensor.matmul_mx(
+                    out=acc1[:],
+                    lhsT=w_codes[:, g, c * P : (c + 1) * P].bitcast(FP8X4),
+                    lhsT_scale=w_planes[:, g, c * P : (c + 1) * P],
+                    rhs=a_codes[:, g, :].bitcast(FP8X4),
+                    rhs_scale=a_scales[:, g, :],
+                    start=(g == 0),
+                    stop=(g == N_PASS - 1),
+                )
+            if chunk < HID_ON_SCALAR:
+                nc.scalar.activation(out=h_f32[:, c, :], in_=acc1[:], func=ACT.Relu, bias=bias[:, c : c + 1])
+                nc.scalar.activation(out=h_sq[:, c, :], in_=h_f32[:, c, :], func=ACT.Square)
+            else:
+                nc.vector.tensor_scalar(
+                    out=h_f32[:, c, :], in0=acc1[:], scalar1=bias[:, c : c + 1], scalar2=0.0,
+                    op0=ALU.add, op1=ALU.max,
+                )
+                nc.vector.tensor_mul(out=h_sq[:, c, :], in0=h_f32[:, c, :], in1=h_f32[:, c, :])
+
+        def quantise_h(chunk):
+            h_f32, h_sq = state["h", chunk]
+            h_grouped = work.tile([P, CHUNK, 4], BF16, tag="h_grouped", align_bytes=64)
+            nc.vector.tensor_copy(out=h_grouped[:], in_=h_f32[:].rearrange("p c b -> p b c"))
+            h_codes = work.tile([P, CHUNK], U32, tag="h_codes", align_bytes=64)
+            h_scales = work.tile([P, CHUNK], U8, tag="h_scales", align_bytes=64)
+            nc.vector.quantize_mx(
+                out=h_codes[:].bitcast(FP8X4),
+                scales=h_scales[:],
+                in_=h_grouped[:].rearrange("p b c -> p (b c)"),
+            )
+            state["hq", chunk] = (h_codes, h_scales)
+
+        def norms_of_h(chunk):
+            h_f32, h_sq = state["h", chunk]
+            hh_ps = psum.tile([P, ROW_TILES, 2], F32, tag="hh")
+            for r in range(ROW_TILES):
+                for k in range(N_HID):
+                    nc.tensor.matmul(
+                        out=hh_ps[:, r, :],
+                        lhsT=h_sq[:, k, r * P : (r + 1) * P],
+                        rhs=ones[:],
+                        start=(k == 0),
+                        stop=(k == N_HID - 1),
+                    )
+            hh_half = work.tile([P, ROW_TILES], F32, tag="hh_half")
+            nc.vector.tensor_scalar(
+                out=hh_half[:], in0=hh_ps[:, :, 0], scalar1=0.5, scalar2=0.5, op0=ALU.mult, op1=ALU.add
+            )
+            state["hh", chunk] = hh_half
+
+        def distances(chunk, r):
+            h_codes, h_scales = state["hq", chunk]
+            hh_half = state["hh", chunk]
+            q = work.tile([P, NY], F32, tag="q", bufs=12)
+            for half in range(N_HALF):
+                cols = slice(512 * half, 512 * (half + 1))
+                acc2 = psum.tile([P, 512], F32, tag="acc2", bufs=2)
+                nc.tensor.matmul_mx(
+                    out=acc2[:],
+                    lhsT=h_codes[:, r * P : (r + 1) * P].bitcast(FP8X4),
+                    lhsT_scale=h_scales[:, r * P : (r + 1) * P],
+                    rhs=wq_codes[:, cols].bitcast(FP8X4),
+                    rhs_scale=wq_scales[:, cols],
+                    start=True,
+                    stop=True,
+                )
+                nc.vector.scalar_tensor_tensor(
+                    out=q[:, cols],
+                    in0=acc2[:],
+                    scalar=hh_half[:, r : r + 1],
+                    in1=ww_half[:, cols],
+                    op0=ALU.subtract,
+                    op1=ALU.subtract,
+                )
+            nc.vector.tensor_scalar_min(out=q[:], in0=q[:], scalar1=-0.5)
+            state["q", chunk, r] = q
+
+        def logs(chunk, r):
+            q = state["q", chunk, r]
+            nc.scalar.activation(out=q[:], in_=q[:], func=ACT.Ln, scale=-2.0)
+
+        def exps(chunk, r):
+            if r == 0:
+                sums = work.tile([P, ROW_TILES], F32, tag="sums")
+                state["sums", chunk] = sums
+            weights = work.tile([P, NY], F32, tag="weights")
+            nc.scalar.activation(
+                out=weights[:],
+                in_=state["q", chunk, r][:],
+                func=ACT.Exp,
+                scale=-1.0,
+                accum_out=state["sums", chunk][:, r : r + 1],
+            )
+
+        def log_of_sums(chunk):
+            lse = work.tile([P, ROW_TILES], F32, tag="lse")
+            nc.scalar.activation(out=lse[:], in_=state["sums", chunk][:], func=ACT.Ln)
+            state["lse", chunk] = lse
+
+        def finish(chunk, r):
+            q = state["q", chunk, r]
+            nc.vector.tensor_scalar(
+                out=q[:], in0=q[:], scalar1=-1.0, scalar2=state["lse", chunk][:, r : r + 1],
+                op0=ALU.mult, op1=ALU.subtract,
+            )
+            rt = chunk * ROW_TILES + r
+            nc.sync.dma_start(out=out[rt * P : (rt + 1) * P, :], in_=q[:])
+
+        n_tiles = B // P
+        relu(0, 0)
+        for rnd in range(n_tiles + LAG_FINISH):
+            if 0 <= rnd - LAG_FINISH < n_tiles:
+                chunk, r = divmod(rnd - LAG_FINISH, ROW_TILES)
+                if r == 0:
+                    log_of_sums(chunk)
+                finish(chunk, r)
+            if 0 <= rnd - LAG_LOGS < n_tiles:
+                chunk, r = divmod(rnd - LAG_LOGS, ROW_TILES)
+                if r < 2:
+                    logs(chunk, 2 * r)
+                    logs(chunk, 2 * r + 1)
+                else:
+                    exps(chunk, 2 * (r - 2))
+                    exps(chunk, 2 * (r - 2) + 1)
+            if 0 <= rnd - LAG_DIST < n_tiles:
+                chunk, r = divmod(rnd - LAG_DIST, ROW_TILES)
+                if r == 0:
+                    norms_of_h(chunk)
+                distances(chunk, r)
+            if 0 <= rnd - LAG_HIDDEN < n_tiles:
+                chunk, c = divmod(rnd - LAG_HIDDEN, N_HID)
+                hidden_chunk(chunk, c)
+                if c == N_HID - 1:
+                    quantise_h(chunk)
+            if rnd < n_tiles:
+                chunk, r = divmod(rnd, ROW_TILES)
+                if rnd + 1 < n_tiles:
+                    relu(*divmod(rnd + 1, ROW_TILES))
+                transpose_row_tile(chunk, r)
+                if r == ROW_TILES - 1:
+                    quantise_a(chunk)
+            if rnd == LAG_HIDDEN - 1:
+                spread_bias()

@@ -22,7 +22,10 @@ ROW_TILES = CHUNK // P
 N_CHUNK = B // CHUNK
 N_HALF = NY // 512
 HID_ON_SCALAR = 2
-LAG_HIDDEN, LAG_DIST, LAG_LOGS, LAG_FINISH = 4, 8, 12, 17
+RELU_AHEAD = 2
+LAG_QUANT_A, LAG_HIDDEN, LAG_QUANT_H, LAG_DIST, LAG_LOGS, LAG_FINISH = 1, 5, 6, 10, 12, 17
+WQ_ROUND = 4
+WW_ROUND = 3
 
 FLOPS = 2 * B * NX * NH + 2 * B * NH * NY
 
@@ -81,8 +84,19 @@ def tile_tnet_kernel(tc, x, W_fc_words, W_fc_scales, b_fc, W_q, out):
 
         ww_col = keep.tile([P, NY // P], F32)
         wq_grouped = keep.tile([P, NY, 4], BF16, align_bytes=64)
-        for pair in range(NY // P // 2):
-            wq_ps = psum.tile([P, 2, 4, P], BF16, tag="xt", bufs=3)
+        wq_codes = keep.tile([P, NY], U32, align_bytes=64)
+        wq_scales = keep.tile([P, NY], U8, align_bytes=64)
+        ww_half = keep.tile([P, NY], F32)
+
+        def norms_of_wq():
+            for a in range(NY // P):
+                squares = work.tile([P, NH], F32, tag="squares")
+                nc.scalar.activation(
+                    out=squares[:], in_=wq_rows[:, a, :], func=ACT.Square, accum_out=ww_col[:, a : a + 1]
+                )
+
+        def transpose_wq(pair):
+            wq_ps = psum.tile([P, 2, 4, P], BF16, tag="bank", bufs=7)
             for a in range(2):
                 for t in range(4):
                     nc.tensor.transpose(
@@ -92,30 +106,26 @@ def tile_tnet_kernel(tc, x, W_fc_words, W_fc_scales, b_fc, W_q, out):
                 out=wq_grouped[:, 2 * pair * P : (2 * pair + 2) * P, :].rearrange("p (a j) t -> p a j t", a=2),
                 in_=wq_ps[:].rearrange("p a t j -> p a j t"),
             )
-        for a in range(NY // P):
-            squares = work.tile([P, NH], F32, tag="squares")
-            nc.scalar.activation(
-                out=squares[:], in_=wq_rows[:, a, :], func=ACT.Square, accum_out=ww_col[:, a : a + 1]
+
+        def quantise_wq():
+            nc.vector.quantize_mx(
+                out=wq_codes[:].bitcast(FP8X4),
+                scales=wq_scales[:],
+                in_=wq_grouped[:].rearrange("p j t -> p (j t)"),
             )
-        wq_codes = keep.tile([P, NY], U32, align_bytes=64)
-        wq_scales = keep.tile([P, NY], U8, align_bytes=64)
-        nc.vector.quantize_mx(
-            out=wq_codes[:].bitcast(FP8X4),
-            scales=wq_scales[:],
-            in_=wq_grouped[:].rearrange("p j t -> p (j t)"),
-        )
-        ww_half = keep.tile([P, NY], F32)
-        for half in range(N_HALF):
-            ww_ps = psum.tile([P, 512], F32, tag="acc2", bufs=2)
-            for a in range(4):
-                nc.tensor.matmul(
-                    out=ww_ps[:, a * P : (a + 1) * P],
-                    lhsT=ww_col[:, 4 * half + a : 4 * half + a + 1].to_broadcast([P, P]),
-                    rhs=ident_f32[:],
-                    start=True,
-                    stop=True,
-                )
-            nc.scalar.mul(out=ww_half[:, 512 * half : 512 * (half + 1)], in_=ww_ps[:], mul=0.5)
+
+        def spread_norms_of_wq():
+            for half in range(N_HALF):
+                ww_ps = psum.tile([P, 512], F32, tag="bank", bufs=7)
+                for a in range(4):
+                    nc.tensor.matmul(
+                        out=ww_ps[:, a * P : (a + 1) * P],
+                        lhsT=ww_col[:, 4 * half + a : 4 * half + a + 1].to_broadcast([P, P]),
+                        rhs=ident_f32[:],
+                        start=True,
+                        stop=True,
+                    )
+                nc.scalar.mul(out=ww_half[:, 512 * half : 512 * (half + 1)], in_=ww_ps[:], mul=0.5)
 
         state = {}
 
@@ -130,7 +140,7 @@ def tile_tnet_kernel(tc, x, W_fc_words, W_fc_scales, b_fc, W_q, out):
             a_words = state["a_grouped", chunk][:].bitcast(F32)
             x_words = x_tiles[chunk * ROW_TILES + r][:].bitcast(F32)
             for pair in range(N_PASS // 2):
-                xt = psum.tile([P, 2, 2, P], F32, tag="xt", bufs=3)
+                xt = psum.tile([P, 2, 2, P], F32, tag="bank", bufs=7)
                 for gi in range(2):
                     g = 2 * pair + gi
                     for u in range(2):
@@ -156,11 +166,11 @@ def tile_tnet_kernel(tc, x, W_fc_words, W_fc_scales, b_fc, W_q, out):
         def hidden_chunk(chunk, c):
             if c == 0:
                 h_f32 = work.tile([P, N_HID, CHUNK], F32, tag="h_f32")
-                h_sq = work.tile([P, N_HID, CHUNK], F32, tag="h_sq")
+                h_sq = work.tile([P, CHUNK], F32, tag="h_sq")
                 state["h", chunk] = (h_f32, h_sq)
             h_f32, h_sq = state["h", chunk]
             a_codes, a_scales = state["a", chunk]
-            acc1 = psum.tile([P, CHUNK], F32, tag="acc1", bufs=2)
+            acc1 = psum.tile([P, CHUNK], F32, tag="bank", bufs=7)
             for g in range(N_PASS):
                 nc.tensor.matmul_mx(
                     out=acc1[:],
@@ -173,13 +183,17 @@ def tile_tnet_kernel(tc, x, W_fc_words, W_fc_scales, b_fc, W_q, out):
                 )
             if chunk < HID_ON_SCALAR:
                 nc.scalar.activation(out=h_f32[:, c, :], in_=acc1[:], func=ACT.Relu, bias=bias[:, c : c + 1])
-                nc.scalar.activation(out=h_sq[:, c, :], in_=h_f32[:, c, :], func=ACT.Square)
             else:
                 nc.vector.tensor_scalar(
                     out=h_f32[:, c, :], in0=acc1[:], scalar1=bias[:, c : c + 1], scalar2=0.0,
                     op0=ALU.add, op1=ALU.max,
                 )
-                nc.vector.tensor_mul(out=h_sq[:, c, :], in0=h_f32[:, c, :], in1=h_f32[:, c, :])
+            if c == 0:
+                nc.gpsimd.tensor_tensor(out=h_sq[:], in0=h_f32[:, c, :], in1=h_f32[:, c, :], op=ALU.mult)
+            else:
+                piece_sq = work.tile([P, CHUNK], F32, tag="piece_sq")
+                nc.gpsimd.tensor_tensor(out=piece_sq[:], in0=h_f32[:, c, :], in1=h_f32[:, c, :], op=ALU.mult)
+                nc.gpsimd.tensor_tensor(out=h_sq[:], in0=h_sq[:], in1=piece_sq[:], op=ALU.add)
 
         def quantise_h(chunk):
             h_f32, h_sq = state["h", chunk]
@@ -198,27 +212,24 @@ def tile_tnet_kernel(tc, x, W_fc_words, W_fc_scales, b_fc, W_q, out):
             h_f32, h_sq = state["h", chunk]
             hh_ps = psum.tile([P, ROW_TILES, 2], F32, tag="hh")
             for r in range(ROW_TILES):
-                for k in range(N_HID):
-                    nc.tensor.matmul(
-                        out=hh_ps[:, r, :],
-                        lhsT=h_sq[:, k, r * P : (r + 1) * P],
-                        rhs=ones[:],
-                        start=(k == 0),
-                        stop=(k == N_HID - 1),
-                    )
+                nc.tensor.matmul(
+                    out=hh_ps[:, r, :], lhsT=h_sq[:, r * P : (r + 1) * P], rhs=ones[:], start=True, stop=True
+                )
+            state["hh_ps", chunk] = hh_ps
+
+        def halve_norms_of_h(chunk):
             hh_half = work.tile([P, ROW_TILES], F32, tag="hh_half")
             nc.vector.tensor_scalar(
-                out=hh_half[:], in0=hh_ps[:, :, 0], scalar1=0.5, scalar2=0.5, op0=ALU.mult, op1=ALU.add
+                out=hh_half[:], in0=state["hh_ps", chunk][:, :, 0], scalar1=0.5, scalar2=0.5,
+                op0=ALU.mult, op1=ALU.add,
             )
             state["hh", chunk] = hh_half
 
-        def distances(chunk, r):
+        def products(chunk, r):
             h_codes, h_scales = state["hq", chunk]
-            hh_half = state["hh", chunk]
-            q = work.tile([P, NY], F32, tag="q", bufs=12)
             for half in range(N_HALF):
                 cols = slice(512 * half, 512 * (half + 1))
-                acc2 = psum.tile([P, 512], F32, tag="acc2", bufs=2)
+                acc2 = psum.tile([P, 512], F32, tag="bank", bufs=7)
                 nc.tensor.matmul_mx(
                     out=acc2[:],
                     lhsT=h_codes[:, r * P : (r + 1) * P].bitcast(FP8X4),
@@ -228,9 +239,16 @@ def tile_tnet_kernel(tc, x, W_fc_words, W_fc_scales, b_fc, W_q, out):
                     start=True,
                     stop=True,
                 )
+                state["acc2", chunk, r, half] = acc2
+
+        def distances(chunk, r):
+            hh_half = state["hh", chunk]
+            q = work.tile([P, NY], F32, tag="q", bufs=12)
+            for half in range(N_HALF):
+                cols = slice(512 * half, 512 * (half + 1))
                 nc.vector.scalar_tensor_tensor(
                     out=q[:, cols],
-                    in0=acc2[:],
+                    in0=state["acc2", chunk, r, half][:],
                     scalar=hh_half[:, r : r + 1],
                     in1=ww_half[:, cols],
                     op0=ALU.subtract,
@@ -271,37 +289,59 @@ def tile_tnet_kernel(tc, x, W_fc_words, W_fc_scales, b_fc, W_q, out):
             nc.sync.dma_start(out=out[rt * P : (rt + 1) * P, :], in_=q[:])
 
         n_tiles = B // P
-        relu(0, 0)
+
+        def due(rnd, lag):
+            return divmod(rnd - lag, ROW_TILES) if 0 <= rnd - lag < n_tiles else None
+
+        def due_chunk(rnd, lag):
+            at = due(rnd, lag)
+            return at[0] if at is not None and at[1] == ROW_TILES - 1 else None
+
+        norms_of_wq()
+        for rt in range(RELU_AHEAD):
+            relu(*divmod(rt, ROW_TILES))
         for rnd in range(n_tiles + LAG_FINISH):
-            if 0 <= rnd - LAG_FINISH < n_tiles:
-                chunk, r = divmod(rnd - LAG_FINISH, ROW_TILES)
-                if r == 0:
-                    log_of_sums(chunk)
-                finish(chunk, r)
-            if 0 <= rnd - LAG_LOGS < n_tiles:
-                chunk, r = divmod(rnd - LAG_LOGS, ROW_TILES)
+            h_chunk = due_chunk(rnd, LAG_QUANT_H)
+            if h_chunk is not None:
+                quantise_h(h_chunk)
+            at = due(rnd, LAG_DIST)
+            if at is not None:
+                products(*at)
+                if at[1] == 0:
+                    halve_norms_of_h(at[0])
+                distances(*at)
+            at = due(rnd, LAG_FINISH)
+            if at is not None:
+                if at[1] == 0:
+                    log_of_sums(at[0])
+                finish(*at)
+            at = due(rnd, LAG_LOGS)
+            if at is not None:
+                chunk, r = at
                 if r < 2:
                     logs(chunk, 2 * r)
                     logs(chunk, 2 * r + 1)
                 else:
                     exps(chunk, 2 * (r - 2))
                     exps(chunk, 2 * (r - 2) + 1)
-            if 0 <= rnd - LAG_DIST < n_tiles:
-                chunk, r = divmod(rnd - LAG_DIST, ROW_TILES)
-                if r == 0:
-                    norms_of_h(chunk)
-                distances(chunk, r)
-            if 0 <= rnd - LAG_HIDDEN < n_tiles:
-                chunk, c = divmod(rnd - LAG_HIDDEN, N_HID)
-                hidden_chunk(chunk, c)
-                if c == N_HID - 1:
-                    quantise_h(chunk)
-            if rnd < n_tiles:
-                chunk, r = divmod(rnd, ROW_TILES)
-                if rnd + 1 < n_tiles:
-                    relu(*divmod(rnd + 1, ROW_TILES))
-                transpose_row_tile(chunk, r)
-                if r == ROW_TILES - 1:
-                    quantise_a(chunk)
+            at = due(rnd, LAG_HIDDEN)
+            if at is not None:
+                hidden_chunk(*at)
+            chunk = due_chunk(rnd, LAG_QUANT_A)
+            if chunk is not None:
+                quantise_a(chunk)
+            if rnd + RELU_AHEAD < n_tiles:
+                relu(*divmod(rnd + RELU_AHEAD, ROW_TILES))
+            at = due(rnd, 0)
+            if at is not None:
+                transpose_row_tile(*at)
+            if h_chunk is not None:
+                norms_of_h(h_chunk)
+            if 0 <= rnd - WQ_ROUND < NY // P // 2:
+                transpose_wq(rnd - WQ_ROUND)
+            if rnd == WQ_ROUND + NY // P // 2 - 1:
+                quantise_wq()
+            if rnd == WW_ROUND:
+                spread_norms_of_wq()
             if rnd == LAG_HIDDEN - 1:
                 spread_bias()

@@ -72,13 +72,11 @@ def tile_tnet_kernel(tc, x, W_fc_words, W_fc_scales, b_fc, W_q, out):
         make_identity(nc, ident_f32[:])
         ident_bf16 = keep.tile([P, P], BF16)
         make_identity(nc, ident_bf16[:])
-        ones = keep.tile([P, 2], F32)
-        nc.vector.memset(ones[:], 1.0)
 
         bias = keep.tile([P, N_HID], F32)
 
         def spread_bias():
-            bias_ps = psum.tile([P, P], BF16, tag="hh")
+            bias_ps = psum.tile([P, P], BF16, tag="bank", bufs=8)
             nc.tensor.transpose(bias_ps[:], bias_rows[:], ident_bf16[:])
             nc.vector.tensor_copy(out=bias[:], in_=bias_ps[:, 0:N_HID])
 
@@ -96,7 +94,7 @@ def tile_tnet_kernel(tc, x, W_fc_words, W_fc_scales, b_fc, W_q, out):
                 )
 
         def transpose_wq(pair):
-            wq_ps = psum.tile([P, 2, 4, P], BF16, tag="bank", bufs=7)
+            wq_ps = psum.tile([P, 2, 4, P], BF16, tag="bank", bufs=8)
             for a in range(2):
                 for t in range(4):
                     nc.tensor.transpose(
@@ -116,7 +114,7 @@ def tile_tnet_kernel(tc, x, W_fc_words, W_fc_scales, b_fc, W_q, out):
 
         def spread_norms_of_wq():
             for half in range(N_HALF):
-                ww_ps = psum.tile([P, 512], F32, tag="bank", bufs=7)
+                ww_ps = psum.tile([P, 512], F32, tag="bank", bufs=8)
                 for a in range(4):
                     nc.tensor.matmul(
                         out=ww_ps[:, a * P : (a + 1) * P],
@@ -140,7 +138,7 @@ def tile_tnet_kernel(tc, x, W_fc_words, W_fc_scales, b_fc, W_q, out):
             a_words = state["a_grouped", chunk][:].bitcast(F32)
             x_words = x_tiles[chunk * ROW_TILES + r][:].bitcast(F32)
             for pair in range(N_PASS // 2):
-                xt = psum.tile([P, 2, 2, P], F32, tag="bank", bufs=7)
+                xt = psum.tile([P, 2, 2, P], F32, tag="bank", bufs=8)
                 for gi in range(2):
                     g = 2 * pair + gi
                     for u in range(2):
@@ -166,11 +164,10 @@ def tile_tnet_kernel(tc, x, W_fc_words, W_fc_scales, b_fc, W_q, out):
         def hidden_chunk(chunk, c):
             if c == 0:
                 h_f32 = work.tile([P, N_HID, CHUNK], F32, tag="h_f32")
-                h_sq = work.tile([P, CHUNK], F32, tag="h_sq")
-                state["h", chunk] = (h_f32, h_sq)
-            h_f32, h_sq = state["h", chunk]
+                state["h", chunk] = h_f32
+            h_f32 = state["h", chunk]
             a_codes, a_scales = state["a", chunk]
-            acc1 = psum.tile([P, CHUNK], F32, tag="bank", bufs=7)
+            acc1 = psum.tile([P, CHUNK], F32, tag="bank", bufs=8)
             for g in range(N_PASS):
                 nc.tensor.matmul_mx(
                     out=acc1[:],
@@ -188,15 +185,9 @@ def tile_tnet_kernel(tc, x, W_fc_words, W_fc_scales, b_fc, W_q, out):
                     out=h_f32[:, c, :], in0=acc1[:], scalar1=bias[:, c : c + 1], scalar2=0.0,
                     op0=ALU.add, op1=ALU.max,
                 )
-            if c == 0:
-                nc.gpsimd.tensor_tensor(out=h_sq[:], in0=h_f32[:, c, :], in1=h_f32[:, c, :], op=ALU.mult)
-            else:
-                piece_sq = work.tile([P, CHUNK], F32, tag="piece_sq")
-                nc.gpsimd.tensor_tensor(out=piece_sq[:], in0=h_f32[:, c, :], in1=h_f32[:, c, :], op=ALU.mult)
-                nc.gpsimd.tensor_tensor(out=h_sq[:], in0=h_sq[:], in1=piece_sq[:], op=ALU.add)
 
         def quantise_h(chunk):
-            h_f32, h_sq = state["h", chunk]
+            h_f32 = state["h", chunk]
             h_grouped = work.tile([P, CHUNK, 4], BF16, tag="h_grouped", align_bytes=64)
             nc.vector.tensor_copy(out=h_grouped[:], in_=h_f32[:].rearrange("p c b -> p b c"))
             h_codes = work.tile([P, CHUNK], U32, tag="h_codes", align_bytes=64)
@@ -209,19 +200,25 @@ def tile_tnet_kernel(tc, x, W_fc_words, W_fc_scales, b_fc, W_q, out):
             state["hq", chunk] = (h_codes, h_scales)
 
         def norms_of_h(chunk):
-            h_f32, h_sq = state["h", chunk]
-            hh_ps = psum.tile([P, ROW_TILES, 2], F32, tag="hh")
+            h_f32 = state["h", chunk]
+            hh = work.tile([P, ROW_TILES], F32, tag="hh")
             for r in range(ROW_TILES):
-                nc.tensor.matmul(
-                    out=hh_ps[:, r, :], lhsT=h_sq[:, r * P : (r + 1) * P], rhs=ones[:], start=True, stop=True
+                h_rows = psum.tile([P, N_HID, P], F32, tag="bank", bufs=8)
+                for k in range(N_HID):
+                    nc.tensor.transpose(h_rows[:, k, :], h_f32[:, k, r * P : (r + 1) * P], ident_f32[:])
+                squares = work.tile([P, NH], F32, tag="squares")
+                nc.scalar.activation(
+                    out=squares[:],
+                    in_=h_rows[:].rearrange("p k n -> p (k n)"),
+                    func=ACT.Square,
+                    accum_out=hh[:, r : r + 1],
                 )
-            state["hh_ps", chunk] = hh_ps
+            state["hh_sum", chunk] = hh
 
         def halve_norms_of_h(chunk):
             hh_half = work.tile([P, ROW_TILES], F32, tag="hh_half")
             nc.vector.tensor_scalar(
-                out=hh_half[:], in0=state["hh_ps", chunk][:, :, 0], scalar1=0.5, scalar2=0.5,
-                op0=ALU.mult, op1=ALU.add,
+                out=hh_half[:], in0=state["hh_sum", chunk][:], scalar1=0.5, scalar2=0.5, op0=ALU.mult, op1=ALU.add
             )
             state["hh", chunk] = hh_half
 
@@ -229,7 +226,7 @@ def tile_tnet_kernel(tc, x, W_fc_words, W_fc_scales, b_fc, W_q, out):
             h_codes, h_scales = state["hq", chunk]
             for half in range(N_HALF):
                 cols = slice(512 * half, 512 * (half + 1))
-                acc2 = psum.tile([P, 512], F32, tag="bank", bufs=7)
+                acc2 = psum.tile([P, 512], F32, tag="bank", bufs=8)
                 nc.tensor.matmul_mx(
                     out=acc2[:],
                     lhsT=h_codes[:, r * P : (r + 1) * P].bitcast(FP8X4),

@@ -22,10 +22,10 @@ ROW_TILES = CHUNK // P
 N_CHUNK = B // CHUNK
 N_HALF = NY // 512
 HID_ON_SCALAR = 2
-RELU_AHEAD = 2
-LAG_QUANT_A, LAG_HIDDEN, LAG_QUANT_H, LAG_DIST, LAG_LOGS, LAG_FINISH = 1, 5, 6, 10, 12, 17
-WQ_ROUND = 4
-WW_ROUND = 3
+PER_ROUND = 2
+LAG_QUANT_A, LAG_HIDDEN, LAG_QUANT_H, LAG_DIST, LAG_LOGS, LAG_FINISH = 1, 3, 4, 6, 8, 10
+WQ_ROUND = 2
+WW_ROUND = 1
 
 FLOPS = 2 * B * NX * NH + 2 * B * NH * NY
 
@@ -240,7 +240,7 @@ def tile_tnet_kernel(tc, x, W_fc_words, W_fc_scales, b_fc, W_q, out):
 
         def distances(chunk, r):
             hh_half = state["hh", chunk]
-            q = work.tile([P, NY], F32, tag="q", bufs=12)
+            q = work.tile([P, NY], F32, tag="q", bufs=14)
             for half in range(N_HALF):
                 cols = slice(512 * half, 512 * (half + 1))
                 nc.vector.scalar_tensor_tensor(
@@ -286,57 +286,56 @@ def tile_tnet_kernel(tc, x, W_fc_words, W_fc_scales, b_fc, W_q, out):
             nc.sync.dma_start(out=out[rt * P : (rt + 1) * P, :], in_=q[:])
 
         n_tiles = B // P
+        n_rounds = n_tiles // PER_ROUND
 
         def due(rnd, lag):
-            return divmod(rnd - lag, ROW_TILES) if 0 <= rnd - lag < n_tiles else None
+            if not 0 <= rnd - lag < n_rounds:
+                return []
+            return [divmod((rnd - lag) * PER_ROUND + t, ROW_TILES) for t in range(PER_ROUND)]
 
         def due_chunk(rnd, lag):
-            at = due(rnd, lag)
-            return at[0] if at is not None and at[1] == ROW_TILES - 1 else None
+            last = [chunk for chunk, r in due(rnd, lag) if r == ROW_TILES - 1]
+            return last[0] if last else None
 
         norms_of_wq()
-        for rt in range(RELU_AHEAD):
+        for rt in range(PER_ROUND):
             relu(*divmod(rt, ROW_TILES))
-        for rnd in range(n_tiles + LAG_FINISH):
+        for rnd in range(n_rounds + LAG_FINISH):
             h_chunk = due_chunk(rnd, LAG_QUANT_H)
             if h_chunk is not None:
                 quantise_h(h_chunk)
-            at = due(rnd, LAG_DIST)
-            if at is not None:
+            for at in due(rnd, LAG_DIST):
                 products(*at)
+            for at in due(rnd, LAG_DIST):
                 if at[1] == 0:
                     halve_norms_of_h(at[0])
                 distances(*at)
-            at = due(rnd, LAG_FINISH)
-            if at is not None:
+            for at in due(rnd, LAG_FINISH):
                 if at[1] == 0:
                     log_of_sums(at[0])
                 finish(*at)
-            at = due(rnd, LAG_LOGS)
-            if at is not None:
-                chunk, r = at
-                if r < 2:
-                    logs(chunk, 2 * r)
-                    logs(chunk, 2 * r + 1)
-                else:
-                    exps(chunk, 2 * (r - 2))
-                    exps(chunk, 2 * (r - 2) + 1)
-            at = due(rnd, LAG_HIDDEN)
-            if at is not None:
+            if 0 <= rnd - LAG_LOGS < 2 * N_CHUNK:
+                chunk, phase = divmod(rnd - LAG_LOGS, 2)
+                for r in range(ROW_TILES):
+                    if phase == 0:
+                        logs(chunk, r)
+                    else:
+                        exps(chunk, r)
+            for at in due(rnd, LAG_HIDDEN):
                 hidden_chunk(*at)
             chunk = due_chunk(rnd, LAG_QUANT_A)
             if chunk is not None:
                 quantise_a(chunk)
-            if rnd + RELU_AHEAD < n_tiles:
-                relu(*divmod(rnd + RELU_AHEAD, ROW_TILES))
-            at = due(rnd, 0)
-            if at is not None:
+            for at in due(rnd + 1, 0):
+                relu(*at)
+            for at in due(rnd, 0):
                 transpose_row_tile(*at)
             if h_chunk is not None:
                 norms_of_h(h_chunk)
-            if 0 <= rnd - WQ_ROUND < NY // P // 2:
-                transpose_wq(rnd - WQ_ROUND)
-            if rnd == WQ_ROUND + NY // P // 2 - 1:
+            if rnd in (WQ_ROUND, WQ_ROUND + 1):
+                transpose_wq(2 * (rnd - WQ_ROUND))
+                transpose_wq(2 * (rnd - WQ_ROUND) + 1)
+            if rnd == WQ_ROUND + 1:
                 quantise_wq()
             if rnd == WW_ROUND:
                 spread_norms_of_wq()

@@ -23,7 +23,7 @@ N_CHUNK = B // CHUNK
 N_HALF = NY // 512
 HID_ON_SCALAR = 2
 PER_ROUND = 2
-LAG_QUANT_A, LAG_HIDDEN, LAG_QUANT_H, LAG_DIST, LAG_LOGS, LAG_FINISH = 1, 3, 4, 6, 8, 10
+LAG_QUANT_A, LAG_HIDDEN, LAG_QUANT_H, LAG_DIST, LAG_LOGS, LAG_FINISH = 1, 3, 4, 6, 7, 9
 WQ_ROUND = 2
 WW_ROUND = 1
 
@@ -314,13 +314,12 @@ def tile_tnet_kernel(tc, x, W_fc_words, W_fc_scales, b_fc, W_q, out):
                 if at[1] == 0:
                     log_of_sums(at[0])
                 finish(*at)
-            if 0 <= rnd - LAG_LOGS < 2 * N_CHUNK:
-                chunk, phase = divmod(rnd - LAG_LOGS, 2)
+            for at in due(rnd, LAG_LOGS):
+                logs(*at)
+            chunk = due_chunk(rnd, LAG_LOGS)
+            if chunk is not None:
                 for r in range(ROW_TILES):
-                    if phase == 0:
-                        logs(chunk, r)
-                    else:
-                        exps(chunk, r)
+                    exps(chunk, r)
             for at in due(rnd, LAG_HIDDEN):
                 hidden_chunk(*at)
             chunk = due_chunk(rnd, LAG_QUANT_A)

@@ -17,15 +17,11 @@ B, NX, NH, NY = 2048, 2048, 512, 1024
 K_PASS = 4 * P
 N_PASS = NX // K_PASS
 N_HID = NH // P
-CHUNK = 512
-ROW_TILES = CHUNK // P
-N_CHUNK = B // CHUNK
+PAIR = 2 * P
+N_ROUND = B // PAIR
 N_HALF = NY // 512
-HID_ON_SCALAR = 2
-PER_ROUND = 2
-LAG_QUANT_A, LAG_HIDDEN, LAG_QUANT_H, LAG_DIST, LAG_LOGS, LAG_FINISH = 1, 3, 4, 6, 7, 9
-WQ_ROUND = 2
-WW_ROUND = 1
+ROOT_HALF = 0.5**0.5
+EXP_GROUPS = ((0, 1, 2), (3, 4, 5), (6,), (7,))
 
 FLOPS = 2 * B * NX * NH + 2 * B * NH * NY
 
@@ -41,31 +37,30 @@ def tile_tnet_kernel(tc, x, W_fc_words, W_fc_scales, b_fc, W_q, out):
         x_tiles = []
 
         def load_x(rt):
-            x_rt = work.tile([P, NX], BF16, tag="x_rt", bufs=8)
+            x_rt = work.tile([P, NX], BF16, tag="x_rt", bufs=16)
             nc.sync.dma_start(out=x_rt[:], in_=x[rt * P : (rt + 1) * P, :])
             x_tiles.append(x_rt)
 
-        wq_rows = keep.tile([P, NY // P, NH], BF16)
-        nc.sync.dma_start(out=wq_rows[:], in_=W_q.rearrange("(a p) k -> p a k", p=P))
-        for rt in range(ROW_TILES):
+        for rt in range(2):
             load_x(rt)
-
         w_planes = keep.tile([P, N_PASS, NH], U8, align_bytes=64)
         nc.vector.memset(w_planes[:].bitcast(I32), 0)
+        bias_rows = keep.tile([P, P], BF16)
+        nc.vector.memset(bias_rows[:], 0.0)
         for quad in range(4):
             nc.sync.dma_start(
                 out=w_planes[32 * quad : 32 * quad + 4, :, :].bitcast(I32),
                 in_=W_fc_scales[:, 4 * quad : 4 * quad + 4, :].rearrange("g r n -> r g n").bitcast(I32),
             )
+        nc.sync.dma_start(out=bias_rows[0:N_HID, :], in_=b_fc.rearrange("(c p) -> c p", p=P))
+        wq_rows = keep.tile([P, NY // P, NH], BF16)
+        nc.sync.dma_start(out=wq_rows[:], in_=W_q.rearrange("(a p) k -> p a k", p=P))
         w_codes = keep.tile([P, N_PASS, NH], U32, align_bytes=64)
         nc.sync.dma_start(
             out=w_codes[:].bitcast(I32),
             in_=W_fc_words.rearrange("g p n t -> p g (n t)").bitcast(I32),
         )
-        bias_rows = keep.tile([P, P], BF16)
-        nc.vector.memset(bias_rows[:], 0.0)
-        nc.sync.dma_start(out=bias_rows[0:N_HID, :], in_=b_fc.rearrange("(c p) -> c p", p=P))
-        for rt in range(ROW_TILES, B // P):
+        for rt in range(2, B // P):
             load_x(rt)
 
         ident_f32 = keep.tile([P, P], F32)
@@ -90,7 +85,8 @@ def tile_tnet_kernel(tc, x, W_fc_words, W_fc_scales, b_fc, W_q, out):
             for a in range(NY // P):
                 squares = work.tile([P, NH], F32, tag="squares")
                 nc.scalar.activation(
-                    out=squares[:], in_=wq_rows[:, a, :], func=ACT.Square, accum_out=ww_col[:, a : a + 1]
+                    out=squares[:], in_=wq_rows[:, a, :], func=ACT.Square, scale=ROOT_HALF,
+                    accum_out=ww_col[:, a : a + 1],
                 )
 
         def transpose_wq(pair):
@@ -113,6 +109,7 @@ def tile_tnet_kernel(tc, x, W_fc_words, W_fc_scales, b_fc, W_q, out):
             )
 
         def spread_norms_of_wq():
+            nc.vector.tensor_scalar_add(out=ww_col[:], in0=ww_col[:], scalar1=0.5)
             for half in range(N_HALF):
                 ww_ps = psum.tile([P, 512], F32, tag="bank", bufs=8)
                 for a in range(4):
@@ -123,220 +120,254 @@ def tile_tnet_kernel(tc, x, W_fc_words, W_fc_scales, b_fc, W_q, out):
                         start=True,
                         stop=True,
                     )
-                nc.scalar.mul(out=ww_half[:, 512 * half : 512 * (half + 1)], in_=ww_ps[:], mul=0.5)
+                nc.scalar.copy(out=ww_half[:, 512 * half : 512 * (half + 1)], in_=ww_ps[:])
 
         state = {}
 
-        def relu(chunk, r):
-            x_rt = x_tiles[chunk * ROW_TILES + r]
-            nc.vector.tensor_scalar_max(out=x_rt[:], in0=x_rt[:], scalar1=0.0)
-
-        def transpose_row_tile(chunk, r):
-            if r == 0:
-                a_grouped = work.tile([P, N_PASS, CHUNK, 4], BF16, tag="a_grouped", align_bytes=64)
-                state["a_grouped", chunk] = a_grouped
-            a_words = state["a_grouped", chunk][:].bitcast(F32)
-            x_words = x_tiles[chunk * ROW_TILES + r][:].bitcast(F32)
+        def transpose_x(rnd, t):
+            x_words = x_tiles[2 * rnd + t][:].bitcast(F32)
+            banks = []
             for pair in range(N_PASS // 2):
                 xt = psum.tile([P, 2, 2, P], F32, tag="bank", bufs=8)
                 for gi in range(2):
                     g = 2 * pair + gi
                     for u in range(2):
                         nc.tensor.transpose(
-                            xt[:, gi, u, :], x_words[:, 256 * g + u : 256 * (g + 1) : 2], ident_f32[:]
+                            xt[:, u, gi, :], x_words[:, 256 * g + u : 256 * (g + 1) : 2], ident_f32[:]
                         )
-                nc.scalar.copy(
-                    out=a_words[:, 2 * pair : 2 * pair + 2, r * P : (r + 1) * P, :],
-                    in_=xt[:].rearrange("p g u i -> p g i u"),
+                banks.append(xt)
+            state["xt", rnd, t] = banks
+
+        def relu_x(rnd, t):
+            if t == 0:
+                a_grouped = work.tile([P, N_PASS, PAIR, 4], BF16, tag="a_grouped", align_bytes=64)
+                state["a_grouped", rnd] = a_grouped
+            for pair in range(N_PASS // 2):
+                nc.vector.tensor_scalar_max(
+                    out=state["a_grouped", rnd][:, 2 * pair : 2 * pair + 2, t * P : (t + 1) * P, :].rearrange(
+                        "p g i (u e) -> p g i u e", e=2
+                    ),
+                    in0=state["xt", rnd, t][pair][:].bitcast(BF16).rearrange("p u g (i e) -> p g i u e", e=2),
+                    scalar1=0.0,
                 )
 
-        def quantise_a(chunk):
-            a_codes = work.tile([P, N_PASS, CHUNK], U32, tag="a_codes", align_bytes=64)
-            a_scales = work.tile([P, N_PASS, CHUNK], U8, tag="a_scales", align_bytes=64)
-            for g in range(N_PASS):
-                nc.vector.quantize_mx(
-                    out=a_codes[:, g, :].bitcast(FP8X4),
-                    scales=a_scales[:, g, :],
-                    in_=state["a_grouped", chunk][:, g, :, :].rearrange("p b t -> p (b t)"),
-                )
-            state["a", chunk] = (a_codes, a_scales)
+        def quantise_a(rnd):
+            a_codes = work.tile([P, N_PASS, PAIR], U32, tag="a_codes", align_bytes=64)
+            a_scales = work.tile([P, N_PASS, PAIR], U8, tag="a_scales", align_bytes=64)
+            nc.vector.quantize_mx(
+                out=a_codes[:].rearrange("p g b -> p (g b)").bitcast(FP8X4),
+                scales=a_scales[:].rearrange("p g b -> p (g b)"),
+                in_=state["a_grouped", rnd][:].rearrange("p g b t -> p (g b t)"),
+            )
+            state["a", rnd] = (a_codes, a_scales)
 
-        def hidden_chunk(chunk, c):
-            if c == 0:
-                h_f32 = work.tile([P, N_HID, CHUNK], F32, tag="h_f32")
-                state["h", chunk] = h_f32
-            h_f32 = state["h", chunk]
-            a_codes, a_scales = state["a", chunk]
-            acc1 = psum.tile([P, CHUNK], F32, tag="bank", bufs=8)
-            for g in range(N_PASS):
-                nc.tensor.matmul_mx(
-                    out=acc1[:],
-                    lhsT=w_codes[:, g, c * P : (c + 1) * P].bitcast(FP8X4),
-                    lhsT_scale=w_planes[:, g, c * P : (c + 1) * P],
-                    rhs=a_codes[:, g, :].bitcast(FP8X4),
-                    rhs_scale=a_scales[:, g, :],
-                    start=(g == 0),
-                    stop=(g == N_PASS - 1),
-                )
-            if chunk < HID_ON_SCALAR:
-                nc.scalar.activation(out=h_f32[:, c, :], in_=acc1[:], func=ACT.Relu, bias=bias[:, c : c + 1])
-            else:
-                nc.vector.tensor_scalar(
-                    out=h_f32[:, c, :], in0=acc1[:], scalar1=bias[:, c : c + 1], scalar2=0.0,
-                    op0=ALU.add, op1=ALU.max,
-                )
+        def hidden_product(rnd):
+            a_codes, a_scales = state["a", rnd]
+            accs = []
+            for pair in range(N_HID // 2):
+                acc1 = psum.tile([P, 2, PAIR], F32, tag="bank", bufs=8)
+                for ci in range(2):
+                    c = 2 * pair + ci
+                    for g in range(N_PASS):
+                        nc.tensor.matmul_mx(
+                            out=acc1[:, ci, :],
+                            lhsT=w_codes[:, g, c * P : (c + 1) * P].bitcast(FP8X4),
+                            lhsT_scale=w_planes[:, g, c * P : (c + 1) * P],
+                            rhs=a_codes[:, g, :].bitcast(FP8X4),
+                            rhs_scale=a_scales[:, g, :],
+                            start=(g == 0),
+                            stop=(g == N_PASS - 1),
+                        )
+                accs.append(acc1)
+            state["acc1", rnd] = accs
 
-        def quantise_h(chunk):
-            h_f32 = state["h", chunk]
-            h_grouped = work.tile([P, CHUNK, 4], BF16, tag="h_grouped", align_bytes=64)
-            nc.vector.tensor_copy(out=h_grouped[:], in_=h_f32[:].rearrange("p c b -> p b c"))
-            h_codes = work.tile([P, CHUNK], U32, tag="h_codes", align_bytes=64)
-            h_scales = work.tile([P, CHUNK], U8, tag="h_scales", align_bytes=64)
+        def hidden_layer(rnd):
+            h_f32 = work.tile([P, N_HID, PAIR], F32, tag="h_f32", bufs=3)
+            for c in range(N_HID):
+                nc.scalar.activation(
+                    out=h_f32[:, c, :], in_=state["acc1", rnd][c // 2][:, c % 2, :], func=ACT.Relu,
+                    bias=bias[:, c : c + 1],
+                )
+            state["h", rnd] = h_f32
+
+        def round_h(rnd):
+            h_grouped = work.tile([P, PAIR, 4], BF16, tag="h_grouped", align_bytes=64)
+            nc.vector.tensor_copy(out=h_grouped[:], in_=state["h", rnd][:].rearrange("p c b -> p b c"))
+            state["h_grouped", rnd] = h_grouped
+
+        def quantise_h(rnd):
+            h_codes = work.tile([P, PAIR], U32, tag="h_codes", align_bytes=64)
+            h_scales = work.tile([P, PAIR], U8, tag="h_scales", align_bytes=64)
             nc.vector.quantize_mx(
                 out=h_codes[:].bitcast(FP8X4),
                 scales=h_scales[:],
-                in_=h_grouped[:].rearrange("p b c -> p (b c)"),
+                in_=state["h_grouped", rnd][:].rearrange("p b c -> p (b c)"),
             )
-            state["hq", chunk] = (h_codes, h_scales)
+            state["hq", rnd] = (h_codes, h_scales)
 
-        def norms_of_h(chunk):
-            h_f32 = state["h", chunk]
-            hh = work.tile([P, ROW_TILES], F32, tag="hh")
-            for r in range(ROW_TILES):
+        def transpose_h(rnd):
+            h_f32 = state["h", rnd]
+            banks = []
+            for t in range(2):
                 h_rows = psum.tile([P, N_HID, P], F32, tag="bank", bufs=8)
                 for k in range(N_HID):
-                    nc.tensor.transpose(h_rows[:, k, :], h_f32[:, k, r * P : (r + 1) * P], ident_f32[:])
+                    nc.tensor.transpose(h_rows[:, k, :], h_f32[:, k, t * P : (t + 1) * P], ident_f32[:])
+                banks.append(h_rows)
+            state["h_rows", rnd] = banks
+
+        def norms_of_h(rnd):
+            hh = work.tile([P, 2], F32, tag="hh", bufs=3)
+            for t in range(2):
                 squares = work.tile([P, NH], F32, tag="squares")
                 nc.scalar.activation(
                     out=squares[:],
-                    in_=h_rows[:].rearrange("p k n -> p (k n)"),
+                    in_=state["h_rows", rnd][t][:].rearrange("p k n -> p (k n)"),
                     func=ACT.Square,
-                    accum_out=hh[:, r : r + 1],
+                    scale=ROOT_HALF,
+                    accum_out=hh[:, t : t + 1],
                 )
-            state["hh_sum", chunk] = hh
+            state["hh", rnd] = hh
 
-        def halve_norms_of_h(chunk):
-            hh_half = work.tile([P, ROW_TILES], F32, tag="hh_half")
-            nc.vector.tensor_scalar(
-                out=hh_half[:], in0=state["hh_sum", chunk][:], scalar1=0.5, scalar2=0.5, op0=ALU.mult, op1=ALU.add
-            )
-            state["hh", chunk] = hh_half
-
-        def products(chunk, r):
-            h_codes, h_scales = state["hq", chunk]
+        def products(rnd, t):
+            h_codes, h_scales = state["hq", rnd]
             for half in range(N_HALF):
                 cols = slice(512 * half, 512 * (half + 1))
                 acc2 = psum.tile([P, 512], F32, tag="bank", bufs=8)
                 nc.tensor.matmul_mx(
                     out=acc2[:],
-                    lhsT=h_codes[:, r * P : (r + 1) * P].bitcast(FP8X4),
-                    lhsT_scale=h_scales[:, r * P : (r + 1) * P],
+                    lhsT=h_codes[:, t * P : (t + 1) * P].bitcast(FP8X4),
+                    lhsT_scale=h_scales[:, t * P : (t + 1) * P],
                     rhs=wq_codes[:, cols].bitcast(FP8X4),
                     rhs_scale=wq_scales[:, cols],
                     start=True,
                     stop=True,
                 )
-                state["acc2", chunk, r, half] = acc2
+                state["acc2", rnd, t, half] = acc2
 
-        def distances(chunk, r):
-            hh_half = state["hh", chunk]
-            q = work.tile([P, NY], F32, tag="q", bufs=14)
+        def distances(rnd, t):
+            q = work.tile([P, NY], F32, tag="q", bufs=16)
             for half in range(N_HALF):
                 cols = slice(512 * half, 512 * (half + 1))
                 nc.vector.scalar_tensor_tensor(
                     out=q[:, cols],
-                    in0=state["acc2", chunk, r, half][:],
-                    scalar=hh_half[:, r : r + 1],
+                    in0=state["acc2", rnd, t, half][:],
+                    scalar=state["hh", rnd][:, t : t + 1],
                     in1=ww_half[:, cols],
                     op0=ALU.subtract,
                     op1=ALU.subtract,
                 )
-            nc.vector.tensor_scalar_min(out=q[:], in0=q[:], scalar1=-0.5)
-            state["q", chunk, r] = q
+            state["q", rnd, t] = q
 
-        def logs(chunk, r):
-            q = state["q", chunk, r]
+        def clamp(rnd, t):
+            q = state["q", rnd, t]
+            nc.vector.tensor_scalar_min(out=q[:], in0=q[:], scalar1=-0.5)
+
+        def logs(rnd, t):
+            q = state["q", rnd, t]
             nc.scalar.activation(out=q[:], in_=q[:], func=ACT.Ln, scale=-2.0)
 
-        def exps(chunk, r):
-            if r == 0:
-                sums = work.tile([P, ROW_TILES], F32, tag="sums")
-                state["sums", chunk] = sums
-            weights = work.tile([P, NY], F32, tag="weights")
-            nc.scalar.activation(
-                out=weights[:],
-                in_=state["q", chunk, r][:],
-                func=ACT.Exp,
-                scale=-1.0,
-                accum_out=state["sums", chunk][:, r : r + 1],
-            )
+        def exps(group, i, t):
+            if (i, t) == (0, 0):
+                sums = work.tile([P, 2 * len(group)], F32, tag="sums" + str(len(group)))
+                state["sums", group] = sums
+            sums = state["sums", group]
+            for rnd in (group[i],):
+                if True:
+                    weights = work.tile([P, NY], F32, tag="weights")
+                    nc.scalar.activation(
+                        out=weights[:],
+                        in_=state["q", rnd, t][:],
+                        func=ACT.Exp,
+                        scale=-1.0,
+                        accum_out=sums[:, 2 * i + t : 2 * i + t + 1],
+                    )
+        def log_of_sums(group):
+            lse = work.tile([P, 2 * len(group)], F32, tag="lse" + str(len(group)))
+            nc.scalar.activation(out=lse[:], in_=state["sums", group][:], func=ACT.Ln)
+            state["lse", group] = lse
 
-        def log_of_sums(chunk):
-            lse = work.tile([P, ROW_TILES], F32, tag="lse")
-            nc.scalar.activation(out=lse[:], in_=state["sums", chunk][:], func=ACT.Ln)
-            state["lse", chunk] = lse
+        def finish(group, i, t):
+            for rnd in (group[i],):
+                if True:
+                    q = state["q", rnd, t]
+                    nc.vector.tensor_scalar(
+                        out=q[:], in0=q[:], scalar1=-1.0, scalar2=state["lse", group][:, 2 * i + t : 2 * i + t + 1],
+                        op0=ALU.mult, op1=ALU.subtract,
+                    )
+                    rt = 2 * rnd + t
+                    nc.sync.dma_start(out=out[rt * P : (rt + 1) * P, :], in_=q[:])
 
-        def finish(chunk, r):
-            q = state["q", chunk, r]
-            nc.vector.tensor_scalar(
-                out=q[:], in0=q[:], scalar1=-1.0, scalar2=state["lse", chunk][:, r : r + 1],
-                op0=ALU.mult, op1=ALU.subtract,
-            )
-            rt = chunk * ROW_TILES + r
-            nc.sync.dma_start(out=out[rt * P : (rt + 1) * P, :], in_=q[:])
-
-        n_tiles = B // P
-        n_rounds = n_tiles // PER_ROUND
-
-        def due(rnd, lag):
-            if not 0 <= rnd - lag < n_rounds:
-                return []
-            return [divmod((rnd - lag) * PER_ROUND + t, ROW_TILES) for t in range(PER_ROUND)]
-
-        def due_chunk(rnd, lag):
-            last = [chunk for chunk, r in due(rnd, lag) if r == ROW_TILES - 1]
-            return last[0] if last else None
-
+        EXP_GROUPS = ((0,1), (2, 3), (4, 5), (6,7))
+        fifo = []
+        for group in EXP_GROUPS:
+            for i, rnd in enumerate(group):
+                fifo += [("L", group, i, 0, rnd), ("L", group, i, 1, rnd)]
+            for i, rnd in enumerate(group):
+                fifo += [("E", group, i, 0, rnd), ("E", group, i, 1, rnd)]
+            fifo.append(("S", group, 0, 0, rnd))
+        fins = []
+        def units(n, step, slot):
+            while n > 0 and fifo:
+                k, group, i, t, rnd = fifo[0]
+                if k == "L" and (rnd + 2 > step or (rnd + 2 == step and slot == 0)):
+                    return
+                if k == "S" and len(fifo) > 1:
+                    r = fifo[1][4]
+                    if (r + 2 > step or (r + 2 == step and slot == 0)):
+                        return
+                fifo.pop(0)
+                if k == "L":
+                    logs(rnd, t)
+                elif k == "E":
+                    exps(group, i, t)
+                else:
+                    log_of_sums(group)
+                    fins.extend((group, j, tt) for j in range(len(group)) for tt in range(2))
+                    continue
+                n -= 1
         norms_of_wq()
-        for rt in range(PER_ROUND):
-            relu(*divmod(rt, ROW_TILES))
-        for rnd in range(n_rounds + LAG_FINISH):
-            h_chunk = due_chunk(rnd, LAG_QUANT_H)
-            if h_chunk is not None:
-                quantise_h(h_chunk)
-            for at in due(rnd, LAG_DIST):
-                products(*at)
-            for at in due(rnd, LAG_DIST):
-                if at[1] == 0:
-                    halve_norms_of_h(at[0])
-                distances(*at)
-            for at in due(rnd, LAG_FINISH):
-                if at[1] == 0:
-                    log_of_sums(at[0])
-                finish(*at)
-            for at in due(rnd, LAG_LOGS):
-                logs(*at)
-            chunk = due_chunk(rnd, LAG_LOGS)
-            if chunk is not None:
-                for r in range(ROW_TILES):
-                    exps(chunk, r)
-            for at in due(rnd, LAG_HIDDEN):
-                hidden_chunk(*at)
-            chunk = due_chunk(rnd, LAG_QUANT_A)
-            if chunk is not None:
-                quantise_a(chunk)
-            for at in due(rnd + 1, 0):
-                relu(*at)
-            for at in due(rnd, 0):
-                transpose_row_tile(*at)
-            if h_chunk is not None:
-                norms_of_h(h_chunk)
-            if rnd in (WQ_ROUND, WQ_ROUND + 1):
-                transpose_wq(2 * (rnd - WQ_ROUND))
-                transpose_wq(2 * (rnd - WQ_ROUND) + 1)
-            if rnd == WQ_ROUND + 1:
-                quantise_wq()
-            if rnd == WW_ROUND:
-                spread_norms_of_wq()
-            if rnd == LAG_HIDDEN - 1:
+        for step in range(N_ROUND + 2):
+            r0, r1, r2 = step, step - 1, step - 2
+            front, middle, back = r0 < N_ROUND, 0 <= r1 < N_ROUND, 0 <= r2 < N_ROUND
+            if step == 1:
                 spread_bias()
+            if middle:
+                hidden_product(r1)
+            if front:
+                transpose_x(r0, 0)
+                transpose_x(r0, 1)
+            if middle:
+                hidden_layer(r1)
+            if step == 1:
+                spread_norms_of_wq()
+            if back:
+                distances(r2, 0)
+                distances(r2, 1)
+                clamp(r2, 0)
+                clamp(r2, 1)
+            units(2, step, 0)
+            if front:
+                relu_x(r0, 0)
+            if middle:
+                transpose_h(r1)
+                norms_of_h(r1)
+                round_h(r1)
+            if front:
+                relu_x(r0, 1)
+            if middle:
+                quantise_h(r1)
+                products(r1, 0)
+                products(r1, 1)
+            if front:
+                quantise_a(r0)
+            if step == 0:
+                for pair in range(4):
+                    transpose_wq(pair)
+                quantise_wq()
+            for _ in range(4):
+                if fins and step < 99:
+                    finish(*fins.pop(0))
+            units(3, step, 1)
+        units(99, 99, 1)
+        for f in fins:
+            finish(*f)

@@ -1,3 +1,4 @@
+import math
 from contextlib import ExitStack
 
 import concourse.mybir as mybir
@@ -17,11 +18,22 @@ B, NX, NH, NY = 2048, 2048, 512, 1024
 K_PASS = 4 * P
 N_PASS = NX // K_PASS
 N_HID = NH // P
-PAIR = 2 * P
-N_ROUND = B // PAIR
+N_TILE = B // P
+ROUNDS = ((0,),) + tuple((i, i + 1) for i in range(1, N_TILE - 2, 2)) + ((N_TILE - 1,),)
 N_HALF = NY // 512
 ROOT_HALF = 0.5**0.5
-EXP_GROUPS = ((0, 1, 2), (3, 4, 5), (6,), (7,))
+LN2 = math.log(2.0)
+
+GROUPS = ((0, 1, 2, 3, 4, 5, 6,), (7, 8, 9, 10, 11, 12,), (13, 14, 15,))
+RELU_ON_SCALAR = tuple(range(2, 5))
+HIDDEN_ON_VECTOR = ()
+X_FIRST = 1
+SLOT_A = 2
+SLOT_B = 3
+PER = 2
+NEWTON = False
+ITS = 3
+FIN = 3
 
 FLOPS = 2 * B * NX * NH + 2 * B * NH * NY
 
@@ -41,7 +53,7 @@ def tile_tnet_kernel(tc, x, W_fc_words, W_fc_scales, b_fc, W_q, out):
             nc.sync.dma_start(out=x_rt[:], in_=x[rt * P : (rt + 1) * P, :])
             x_tiles.append(x_rt)
 
-        for rt in range(2):
+        for rt in range(X_FIRST):
             load_x(rt)
         w_planes = keep.tile([P, N_PASS, NH], U8, align_bytes=64)
         nc.vector.memset(w_planes[:].bitcast(I32), 0)
@@ -60,7 +72,7 @@ def tile_tnet_kernel(tc, x, W_fc_words, W_fc_scales, b_fc, W_q, out):
             out=w_codes[:].bitcast(I32),
             in_=W_fc_words.rearrange("g p n t -> p g (n t)").bitcast(I32),
         )
-        for rt in range(2, B // P):
+        for rt in range(len(x_tiles), N_TILE):
             load_x(rt)
 
         ident_f32 = keep.tile([P, P], F32)
@@ -80,6 +92,10 @@ def tile_tnet_kernel(tc, x, W_fc_words, W_fc_scales, b_fc, W_q, out):
         wq_codes = keep.tile([P, NY], U32, align_bytes=64)
         wq_scales = keep.tile([P, NY], U8, align_bytes=64)
         ww_half = keep.tile([P, NY], F32)
+
+        one = keep.tile([P, 1], F32)
+        nc.vector.memset(one[:], 1.0)
+        nc.scalar.activation(out=one[:], in_=one[:], func=ACT.Ln)
 
         def norms_of_wq():
             for a in range(NY // P):
@@ -125,7 +141,7 @@ def tile_tnet_kernel(tc, x, W_fc_words, W_fc_scales, b_fc, W_q, out):
         state = {}
 
         def transpose_x(rnd, t):
-            x_words = x_tiles[2 * rnd + t][:].bitcast(F32)
+            x_words = x_tiles[ROUNDS[rnd][t]][:].bitcast(F32)
             banks = []
             for pair in range(N_PASS // 2):
                 xt = psum.tile([P, 2, 2, P], F32, tag="bank", bufs=8)
@@ -140,20 +156,22 @@ def tile_tnet_kernel(tc, x, W_fc_words, W_fc_scales, b_fc, W_q, out):
 
         def relu_x(rnd, t):
             if t == 0:
-                a_grouped = work.tile([P, N_PASS, PAIR, 4], BF16, tag="a_grouped", align_bytes=64)
+                a_grouped = work.tile([P, N_PASS, len(ROUNDS[rnd]) * P, 4], BF16, tag="a_grouped", align_bytes=64)
                 state["a_grouped", rnd] = a_grouped
             for pair in range(N_PASS // 2):
-                nc.vector.tensor_scalar_max(
-                    out=state["a_grouped", rnd][:, 2 * pair : 2 * pair + 2, t * P : (t + 1) * P, :].rearrange(
-                        "p g i (u e) -> p g i u e", e=2
-                    ),
-                    in0=state["xt", rnd, t][pair][:].bitcast(BF16).rearrange("p u g (i e) -> p g i u e", e=2),
-                    scalar1=0.0,
+                grouped = state["a_grouped", rnd][:, 2 * pair : 2 * pair + 2, t * P : (t + 1) * P, :].rearrange(
+                    "p g i (u e) -> p g i u e", e=2
                 )
+                bank = state["xt", rnd, t][pair][:].bitcast(BF16).rearrange("p u g (i e) -> p g i u e", e=2)
+                if t == 0 and rnd in RELU_ON_SCALAR:
+                    nc.scalar.activation(out=grouped, in_=bank, func=ACT.Relu)
+                else:
+                    nc.vector.tensor_scalar_max(out=grouped, in0=bank, scalar1=0.0)
 
         def quantise_a(rnd):
-            a_codes = work.tile([P, N_PASS, PAIR], U32, tag="a_codes", align_bytes=64)
-            a_scales = work.tile([P, N_PASS, PAIR], U8, tag="a_scales", align_bytes=64)
+            n = len(ROUNDS[rnd]) * P
+            a_codes = work.tile([P, N_PASS, n], U32, tag="a_codes", align_bytes=64)
+            a_scales = work.tile([P, N_PASS, n], U8, tag="a_scales", align_bytes=64)
             nc.vector.quantize_mx(
                 out=a_codes[:].rearrange("p g b -> p (g b)").bitcast(FP8X4),
                 scales=a_scales[:].rearrange("p g b -> p (g b)"),
@@ -162,42 +180,49 @@ def tile_tnet_kernel(tc, x, W_fc_words, W_fc_scales, b_fc, W_q, out):
             state["a", rnd] = (a_codes, a_scales)
 
         def hidden_product(rnd):
+            n = len(ROUNDS[rnd]) * P
             a_codes, a_scales = state["a", rnd]
+            per_bank = 512 // n
             accs = []
-            for pair in range(N_HID // 2):
-                acc1 = psum.tile([P, 2, PAIR], F32, tag="bank", bufs=8)
-                for ci in range(2):
-                    c = 2 * pair + ci
-                    for g in range(N_PASS):
-                        nc.tensor.matmul_mx(
-                            out=acc1[:, ci, :],
-                            lhsT=w_codes[:, g, c * P : (c + 1) * P].bitcast(FP8X4),
-                            lhsT_scale=w_planes[:, g, c * P : (c + 1) * P],
-                            rhs=a_codes[:, g, :].bitcast(FP8X4),
-                            rhs_scale=a_scales[:, g, :],
-                            start=(g == 0),
-                            stop=(g == N_PASS - 1),
-                        )
-                accs.append(acc1)
+            for c in range(N_HID):
+                if c % per_bank == 0:
+                    acc1 = psum.tile([P, per_bank, n], F32, tag="bank", bufs=8)
+                for g in range(N_PASS):
+                    nc.tensor.matmul_mx(
+                        out=acc1[:, c % per_bank, :],
+                        lhsT=w_codes[:, g, c * P : (c + 1) * P].bitcast(FP8X4),
+                        lhsT_scale=w_planes[:, g, c * P : (c + 1) * P],
+                        rhs=a_codes[:, g, :].bitcast(FP8X4),
+                        rhs_scale=a_scales[:, g, :],
+                        start=(g == 0),
+                        stop=(g == N_PASS - 1),
+                    )
+                accs.append(acc1[:, c % per_bank, :])
             state["acc1", rnd] = accs
 
         def hidden_layer(rnd):
-            h_f32 = work.tile([P, N_HID, PAIR], F32, tag="h_f32", bufs=3)
+            h_f32 = work.tile([P, N_HID, len(ROUNDS[rnd]) * P], F32, tag="h_f32", bufs=3)
             for c in range(N_HID):
-                nc.scalar.activation(
-                    out=h_f32[:, c, :], in_=state["acc1", rnd][c // 2][:, c % 2, :], func=ACT.Relu,
-                    bias=bias[:, c : c + 1],
-                )
+                if rnd in HIDDEN_ON_VECTOR:
+                    nc.vector.tensor_scalar(
+                        out=h_f32[:, c, :], in0=state["acc1", rnd][c], scalar1=bias[:, c : c + 1], scalar2=0.0,
+                        op0=ALU.add, op1=ALU.max,
+                    )
+                else:
+                    nc.scalar.activation(
+                        out=h_f32[:, c, :], in_=state["acc1", rnd][c], func=ACT.Relu, bias=bias[:, c : c + 1]
+                    )
             state["h", rnd] = h_f32
 
         def round_h(rnd):
-            h_grouped = work.tile([P, PAIR, 4], BF16, tag="h_grouped", align_bytes=64)
+            h_grouped = work.tile([P, len(ROUNDS[rnd]) * P, 4], BF16, tag="h_grouped", align_bytes=64)
             nc.vector.tensor_copy(out=h_grouped[:], in_=state["h", rnd][:].rearrange("p c b -> p b c"))
             state["h_grouped", rnd] = h_grouped
 
         def quantise_h(rnd):
-            h_codes = work.tile([P, PAIR], U32, tag="h_codes", align_bytes=64)
-            h_scales = work.tile([P, PAIR], U8, tag="h_scales", align_bytes=64)
+            n = len(ROUNDS[rnd]) * P
+            h_codes = work.tile([P, n], U32, tag="h_codes", align_bytes=64)
+            h_scales = work.tile([P, n], U8, tag="h_scales", align_bytes=64)
             nc.vector.quantize_mx(
                 out=h_codes[:].bitcast(FP8X4),
                 scales=h_scales[:],
@@ -208,7 +233,7 @@ def tile_tnet_kernel(tc, x, W_fc_words, W_fc_scales, b_fc, W_q, out):
         def transpose_h(rnd):
             h_f32 = state["h", rnd]
             banks = []
-            for t in range(2):
+            for t in range(len(ROUNDS[rnd])):
                 h_rows = psum.tile([P, N_HID, P], F32, tag="bank", bufs=8)
                 for k in range(N_HID):
                     nc.tensor.transpose(h_rows[:, k, :], h_f32[:, k, t * P : (t + 1) * P], ident_f32[:])
@@ -217,7 +242,7 @@ def tile_tnet_kernel(tc, x, W_fc_words, W_fc_scales, b_fc, W_q, out):
 
         def norms_of_h(rnd):
             hh = work.tile([P, 2], F32, tag="hh", bufs=3)
-            for t in range(2):
+            for t in range(len(ROUNDS[rnd])):
                 squares = work.tile([P, NH], F32, tag="squares")
                 nc.scalar.activation(
                     out=squares[:],
@@ -228,146 +253,175 @@ def tile_tnet_kernel(tc, x, W_fc_words, W_fc_scales, b_fc, W_q, out):
                 )
             state["hh", rnd] = hh
 
-        def products(rnd, t):
+        def products(rnd):
             h_codes, h_scales = state["hq", rnd]
-            for half in range(N_HALF):
-                cols = slice(512 * half, 512 * (half + 1))
-                acc2 = psum.tile([P, 512], F32, tag="bank", bufs=8)
-                nc.tensor.matmul_mx(
-                    out=acc2[:],
-                    lhsT=h_codes[:, t * P : (t + 1) * P].bitcast(FP8X4),
-                    lhsT_scale=h_scales[:, t * P : (t + 1) * P],
-                    rhs=wq_codes[:, cols].bitcast(FP8X4),
-                    rhs_scale=wq_scales[:, cols],
-                    start=True,
-                    stop=True,
-                )
-                state["acc2", rnd, t, half] = acc2
+            for t in range(len(ROUNDS[rnd])):
+                for half in range(N_HALF):
+                    cols = slice(512 * half, 512 * (half + 1))
+                    acc2 = psum.tile([P, 512], F32, tag="bank", bufs=8)
+                    nc.tensor.matmul_mx(
+                        out=acc2[:],
+                        lhsT=h_codes[:, t * P : (t + 1) * P].bitcast(FP8X4),
+                        lhsT_scale=h_scales[:, t * P : (t + 1) * P],
+                        rhs=wq_codes[:, cols].bitcast(FP8X4),
+                        rhs_scale=wq_scales[:, cols],
+                        start=True,
+                        stop=True,
+                    )
+                    state["acc2", rnd, t, half] = acc2
 
-        def distances(rnd, t):
-            q = work.tile([P, NY], F32, tag="q", bufs=16)
-            for half in range(N_HALF):
-                cols = slice(512 * half, 512 * (half + 1))
-                nc.vector.scalar_tensor_tensor(
-                    out=q[:, cols],
-                    in0=state["acc2", rnd, t, half][:],
-                    scalar=state["hh", rnd][:, t : t + 1],
-                    in1=ww_half[:, cols],
-                    op0=ALU.subtract,
-                    op1=ALU.subtract,
-                )
-            state["q", rnd, t] = q
+        def distances(rnd):
+            for t, rt in enumerate(ROUNDS[rnd]):
+                q = work.tile([P, NY], F32, tag="q", bufs=16)
+                for half in range(N_HALF):
+                    cols = slice(512 * half, 512 * (half + 1))
+                    nc.vector.scalar_tensor_tensor(
+                        out=q[:, cols],
+                        in0=state["acc2", rnd, t, half][:],
+                        scalar=state["hh", rnd][:, t : t + 1],
+                        in1=ww_half[:, cols],
+                        op0=ALU.subtract,
+                        op1=ALU.subtract,
+                    )
+                state["q", rt] = q
 
-        def clamp(rnd, t):
-            q = state["q", rnd, t]
-            nc.vector.tensor_scalar_min(out=q[:], in0=q[:], scalar1=-0.5)
+        def clamp(rnd):
+            for rt in ROUNDS[rnd]:
+                q = state["q", rt]
+                nc.vector.tensor_scalar_min(out=q[:], in0=q[:], scalar1=-0.5)
 
-        def logs(rnd, t):
-            q = state["q", rnd, t]
+        def log_tile(rt):
+            q = state["q", rt]
             nc.scalar.activation(out=q[:], in_=q[:], func=ACT.Ln, scale=-2.0)
 
-        def exps(group, i, t):
-            if (i, t) == (0, 0):
-                sums = work.tile([P, 2 * len(group)], F32, tag="sums" + str(len(group)))
-                state["sums", group] = sums
-            sums = state["sums", group]
-            for rnd in (group[i],):
-                if True:
-                    weights = work.tile([P, NY], F32, tag="weights")
-                    nc.scalar.activation(
-                        out=weights[:],
-                        in_=state["q", rnd, t][:],
-                        func=ACT.Exp,
-                        scale=-1.0,
-                        accum_out=sums[:, 2 * i + t : 2 * i + t + 1],
-                    )
-        def log_of_sums(group):
-            lse = work.tile([P, 2 * len(group)], F32, tag="lse" + str(len(group)))
-            nc.scalar.activation(out=lse[:], in_=state["sums", group][:], func=ACT.Ln)
-            state["lse", group] = lse
+        def exp_tile(rt, column):
+            weights = work.tile([P, NY], F32, tag="weights")
+            nc.scalar.activation(
+                out=weights[:], in_=state["q", rt][:], func=ACT.Exp, scale=-1.0, accum_out=column
+            )
 
-        def finish(group, i, t):
-            for rnd in (group[i],):
-                if True:
-                    q = state["q", rnd, t]
-                    nc.vector.tensor_scalar(
-                        out=q[:], in0=q[:], scalar1=-1.0, scalar2=state["lse", group][:, 2 * i + t : 2 * i + t + 1],
-                        op0=ALU.mult, op1=ALU.subtract,
-                    )
-                    rt = 2 * rnd + t
-                    nc.sync.dma_start(out=out[rt * P : (rt + 1) * P, :], in_=q[:])
+        def guess_of_log(rnd_sums, y):
+            nc.vector.tensor_scalar(
+                out=y, in0=rnd_sums.bitcast(I32), scalar1=LN2 / 2.0**23, scalar2=(0.043 - 127.0) * LN2,
+                op0=ALU.mult, op1=ALU.add,
+            )
 
-        EXP_GROUPS = ((0,1), (2, 3), (4, 5), (6,7))
-        fifo = []
-        for group in EXP_GROUPS:
-            for i, rnd in enumerate(group):
-                fifo += [("L", group, i, 0, rnd), ("L", group, i, 1, rnd)]
-            for i, rnd in enumerate(group):
-                fifo += [("E", group, i, 0, rnd), ("E", group, i, 1, rnd)]
-            fifo.append(("S", group, 0, 0, rnd))
-        fins = []
-        def units(n, step, slot):
-            while n > 0 and fifo:
-                k, group, i, t, rnd = fifo[0]
-                if k == "L" and (rnd + 2 > step or (rnd + 2 == step and slot == 0)):
+        def newton_exp(y, e):
+            nc.scalar.activation(out=e, in_=y, func=ACT.Exp, scale=-1.0)
+
+        def newton_update(rnd_sums, y, e):
+            nc.vector.tensor_tensor(out=e, in0=e, in1=rnd_sums, op=ALU.mult)
+            nc.vector.scalar_tensor_tensor(out=y, in0=e, scalar=-1.0, in1=y, op0=ALU.add, op1=ALU.add)
+
+        def finish(rt, lse):
+            q = state["q", rt]
+            nc.vector.tensor_scalar(
+                out=q[:], in0=q[:], scalar1=-1.0, scalar2=lse, op0=ALU.mult, op1=ALU.subtract
+            )
+            nc.sync.dma_start(out=out[rt * P : (rt + 1) * P, :], in_=q[:])
+
+        n_rounds = len(ROUNDS)
+        round_of = {rt: rnd for rnd, tiles in enumerate(ROUNDS) for rt in tiles}
+        steps_of_scalar = []
+        for group in GROUPS:
+            steps_of_scalar += [("log", rt, group) for rt in group]
+            steps_of_scalar += [("exp", rt, group) for rt in group]
+            if group != GROUPS[-1] or not NEWTON:
+                steps_of_scalar.append(("sum", group[-1], group))
+        unfinished = []
+        small = []
+
+        def start_lse(sums, tiles):
+            n = len(tiles)
+            y = work.tile([P, n], F32, tag="y" + str(n), bufs=4)
+            e = work.tile([P, n], F32, tag="e" + str(n), bufs=4)
+            small.append(lambda: guess_of_log(sums, y[:]))
+            for _ in range(ITS):
+                small.append(lambda: newton_exp(y[:], e[:]))
+                small.append(lambda: newton_update(sums, y[:], e[:]))
+            small.append(lambda: unfinished.extend((rt, y[:, i : i + 1]) for i, rt in enumerate(tiles)))
+
+        def little(n=1):
+            for piece in small[:n]:
+                piece()
+            for piece in small[:n]:
+                small.remove(piece)
+
+        def advance(n, newest):
+            while n > 0 and steps_of_scalar:
+                kind, rt, group = steps_of_scalar[0]
+                nxt = steps_of_scalar[1][1] if kind == "sum" and len(steps_of_scalar) > 1 else rt
+                if kind != "exp" and round_of[nxt] > newest:
                     return
-                if k == "S" and len(fifo) > 1:
-                    r = fifo[1][4]
-                    if (r + 2 > step or (r + 2 == step and slot == 0)):
-                        return
-                fifo.pop(0)
-                if k == "L":
-                    logs(rnd, t)
-                elif k == "E":
-                    exps(group, i, t)
+                steps_of_scalar.pop(0)
+                i = group.index(rt)
+                if kind == "sum":
+                    lse = work.tile([P, len(group)], F32, tag="lse" + str(len(group)))
+                    nc.scalar.activation(out=lse[:], in_=state["sums", group][:], func=ACT.Ln)
+                    unfinished.extend((rt2, lse[:, i2 : i2 + 1]) for i2, rt2 in enumerate(group))
+                elif kind == "log":
+                    log_tile(rt)
                 else:
-                    log_of_sums(group)
-                    fins.extend((group, j, tt) for j in range(len(group)) for tt in range(2))
-                    continue
+                    if i == 0:
+                        sums = work.tile([P, len(group)], F32, tag="sums" + str(len(group)))
+                        state["sums", group] = sums
+                    exp_tile(rt, state["sums", group][:, i : i + 1])
+                    if NEWTON and group == GROUPS[-1] and ((i + 1) % PER == 0 or i == len(group) - 1):
+                        j = i // PER * PER
+                        start_lse(state["sums", group][:, j : i + 1], group[j : i + 1])
+                little()
                 n -= 1
+
+        def finish_some(n):
+            for tile_and_lse in unfinished[:n]:
+                finish(*tile_and_lse)
+            for done in unfinished[:n]:
+                unfinished.remove(done)
+
         norms_of_wq()
-        for step in range(N_ROUND + 2):
+        for step in range(n_rounds + 2):
             r0, r1, r2 = step, step - 1, step - 2
-            front, middle, back = r0 < N_ROUND, 0 <= r1 < N_ROUND, 0 <= r2 < N_ROUND
+            front, middle, back = r0 < n_rounds, 0 <= r1 < n_rounds, 0 <= r2 < n_rounds
             if step == 1:
                 spread_bias()
             if middle:
                 hidden_product(r1)
             if front:
-                transpose_x(r0, 0)
-                transpose_x(r0, 1)
-            if middle:
+                for t in range(len(ROUNDS[r0])):
+                    transpose_x(r0, t)
+            if middle and r1 not in HIDDEN_ON_VECTOR:
                 hidden_layer(r1)
             if step == 1:
                 spread_norms_of_wq()
             if back:
-                distances(r2, 0)
-                distances(r2, 1)
-                clamp(r2, 0)
-                clamp(r2, 1)
-            units(2, step, 0)
+                distances(r2)
+                clamp(r2)
+            if middle and r1 in HIDDEN_ON_VECTOR:
+                hidden_layer(r1)
+            advance(SLOT_A, r2 - 1)
             if front:
                 relu_x(r0, 0)
             if middle:
                 transpose_h(r1)
                 norms_of_h(r1)
                 round_h(r1)
-            if front:
+            if front and len(ROUNDS[r0]) > 1:
                 relu_x(r0, 1)
             if middle:
                 quantise_h(r1)
-                products(r1, 0)
-                products(r1, 1)
+                products(r1)
             if front:
                 quantise_a(r0)
             if step == 0:
                 for pair in range(4):
                     transpose_wq(pair)
                 quantise_wq()
-            for _ in range(4):
-                if fins and step < 99:
-                    finish(*fins.pop(0))
-            units(3, step, 1)
-        units(99, 99, 1)
-        for f in fins:
-            finish(*f)
+            finish_some(FIN)
+            advance(SLOT_B, r2)
+        while steps_of_scalar:
+            advance(1, n_rounds)
+            little()
+            finish_some(2)
+        while small or unfinished:
+            little()
+            finish_some(2)

@@ -144,12 +144,12 @@ def tile_tnet_kernel(tc, x, W_fc_words, W_fc_scales, b_fc, W_q, out):
             x_words = x_tiles[ROUNDS[rnd][t]][:].bitcast(F32)
             banks = []
             for pair in range(N_PASS // 2):
-                xt = psum.tile([P, 2, 2, P], F32, tag="bank", bufs=8)
+                xt = psum.tile([P, 2, P, 2], F32, tag="bank", bufs=8)
                 for gi in range(2):
                     g = 2 * pair + gi
                     for u in range(2):
                         nc.tensor.transpose(
-                            xt[:, u, gi, :], x_words[:, 256 * g + u : 256 * (g + 1) : 2], ident_f32[:]
+                            xt[:, gi, :, u], x_words[:, 256 * g + u : 256 * (g + 1) : 2], ident_f32[:]
                         )
                 banks.append(xt)
             state["xt", rnd, t] = banks
@@ -159,10 +159,8 @@ def tile_tnet_kernel(tc, x, W_fc_words, W_fc_scales, b_fc, W_q, out):
                 a_grouped = work.tile([P, N_PASS, len(ROUNDS[rnd]) * P, 4], BF16, tag="a_grouped", align_bytes=64)
                 state["a_grouped", rnd] = a_grouped
             for pair in range(N_PASS // 2):
-                grouped = state["a_grouped", rnd][:, 2 * pair : 2 * pair + 2, t * P : (t + 1) * P, :].rearrange(
-                    "p g i (u e) -> p g i u e", e=2
-                )
-                bank = state["xt", rnd, t][pair][:].bitcast(BF16).rearrange("p u g (i e) -> p g i u e", e=2)
+                grouped = state["a_grouped", rnd][:, 2 * pair : 2 * pair + 2, t * P : (t + 1) * P, :]
+                bank = state["xt", rnd, t][pair][:].bitcast(BF16)
                 if t == 0 and rnd in RELU_ON_SCALAR:
                     nc.scalar.activation(out=grouped, in_=bank, func=ACT.Relu)
                 else:

@@ -26,14 +26,16 @@ LN2 = math.log(2.0)
 
 GROUPS = ((0, 1, 2, 3, 4, 5, 6,), (7, 8, 9, 10, 11, 12,), (13, 14, 15,))
 RELU_ON_SCALAR = tuple(range(2, 5))
-HIDDEN_ON_VECTOR = ()
+HIDDEN_ON_VECTOR = (7, 8)
 X_FIRST = 1
 SLOT_A = 2
 SLOT_B = 3
 PER = 2
 NEWTON = False
 ITS = 3
-FIN = 3
+FIN = 0
+WQ_ON_SCALAR = (1, 3)
+WQSQ_FIRST = 4
 
 FLOPS = 2 * B * NX * NH + 2 * B * NH * NY
 
@@ -95,10 +97,11 @@ def tile_tnet_kernel(tc, x, W_fc_words, W_fc_scales, b_fc, W_q, out):
 
         one = keep.tile([P, 1], F32)
         nc.vector.memset(one[:], 1.0)
-        nc.scalar.activation(out=one[:], in_=one[:], func=ACT.Ln)
+        zero = keep.tile([P, 1], F32)
+        nc.scalar.activation(out=zero[:], in_=one[:], func=ACT.Ln)
 
-        def norms_of_wq():
-            for a in range(NY // P):
+        def norms_of_wq(first, last):
+            for a in range(first, last):
                 squares = work.tile([P, NH], F32, tag="squares")
                 nc.scalar.activation(
                     out=squares[:], in_=wq_rows[:, a, :], func=ACT.Square, scale=ROOT_HALF,
@@ -112,10 +115,11 @@ def tile_tnet_kernel(tc, x, W_fc_words, W_fc_scales, b_fc, W_q, out):
                     nc.tensor.transpose(
                         wq_ps[:, a, t, :], wq_rows[:, 2 * pair + a, t * P : (t + 1) * P], ident_bf16[:]
                     )
-            nc.vector.tensor_copy(
-                out=wq_grouped[:, 2 * pair * P : (2 * pair + 2) * P, :].rearrange("p (a j) t -> p a j t", a=2),
-                in_=wq_ps[:].rearrange("p a t j -> p a j t"),
-            )
+            grouped = wq_grouped[:, 2 * pair * P : (2 * pair + 2) * P, :].rearrange("p (a j) t -> p a j t", a=2)
+            if pair in WQ_ON_SCALAR:
+                nc.scalar.copy(out=grouped, in_=wq_ps[:].rearrange("p a t j -> p a j t"))
+            else:
+                nc.vector.tensor_copy(out=grouped, in_=wq_ps[:].rearrange("p a t j -> p a j t"))
 
         def quantise_wq():
             nc.vector.quantize_mx(
@@ -125,7 +129,6 @@ def tile_tnet_kernel(tc, x, W_fc_words, W_fc_scales, b_fc, W_q, out):
             )
 
         def spread_norms_of_wq():
-            nc.vector.tensor_scalar_add(out=ww_col[:], in0=ww_col[:], scalar1=0.5)
             for half in range(N_HALF):
                 ww_ps = psum.tile([P, 512], F32, tag="bank", bufs=8)
                 for a in range(4):
@@ -286,11 +289,11 @@ def tile_tnet_kernel(tc, x, W_fc_words, W_fc_scales, b_fc, W_q, out):
         def clamp(rnd):
             for rt in ROUNDS[rnd]:
                 q = state["q", rt]
-                nc.vector.tensor_scalar_min(out=q[:], in0=q[:], scalar1=-0.5)
+                nc.vector.tensor_scalar_min(out=q[:], in0=q[:], scalar1=0.0)
 
         def log_tile(rt):
             q = state["q", rt]
-            nc.scalar.activation(out=q[:], in_=q[:], func=ACT.Ln, scale=-2.0)
+            nc.scalar.activation(out=q[:], in_=q[:], func=ACT.Ln, scale=-2.0, bias=one[:])
 
         def exp_tile(rt, column):
             weights = work.tile([P, NY], F32, tag="weights")
@@ -376,12 +379,10 @@ def tile_tnet_kernel(tc, x, W_fc_words, W_fc_scales, b_fc, W_q, out):
             for done in unfinished[:n]:
                 unfinished.remove(done)
 
-        norms_of_wq()
+        norms_of_wq(0, WQSQ_FIRST)
         for step in range(n_rounds + 2):
             r0, r1, r2 = step, step - 1, step - 2
             front, middle, back = r0 < n_rounds, 0 <= r1 < n_rounds, 0 <= r2 < n_rounds
-            if step == 1:
-                spread_bias()
             if middle:
                 hidden_product(r1)
             if front:
@@ -390,6 +391,7 @@ def tile_tnet_kernel(tc, x, W_fc_words, W_fc_scales, b_fc, W_q, out):
             if middle and r1 not in HIDDEN_ON_VECTOR:
                 hidden_layer(r1)
             if step == 1:
+                norms_of_wq(WQSQ_FIRST, 8)
                 spread_norms_of_wq()
             if back:
                 distances(r2)
@@ -411,6 +413,7 @@ def tile_tnet_kernel(tc, x, W_fc_words, W_fc_scales, b_fc, W_q, out):
             if front:
                 quantise_a(r0)
             if step == 0:
+                spread_bias()
                 for pair in range(4):
                     transpose_wq(pair)
                 quantise_wq()

@@ -24,18 +24,21 @@ N_HALF = NY // 512
 ROOT_HALF = 0.5**0.5
 LN2 = math.log(2.0)
 
-GROUPS = ((0, 1, 2, 3, 4, 5, 6,), (7, 8, 9, 10, 11, 12,), (13, 14, 15,))
-RELU_ON_SCALAR = tuple(range(2, 5))
-HIDDEN_ON_VECTOR = (7, 8)
+GROUPS = ((0, 1, 2, 3, 4, 5, 6, 7, 8,), (9, 10, 11, 12, 13, 14, 15,))
+RELU_ON_SCALAR = tuple(range(2, 7))
+HIDDEN_ON_VECTOR = (6, 7, 8)
 X_FIRST = 1
 SLOT_A = 2
 SLOT_B = 3
-PER = 2
-NEWTON = False
-ITS = 3
-FIN = 0
-WQ_ON_SCALAR = (1, 3)
-WQSQ_FIRST = 4
+NEWTON = 3
+FIN = 3
+WARM_0 = 0
+WARM_1 = 0
+WARM_2 = 0
+WARM_3 = 0
+WARM_4 = 0
+WQ_ON_SCALAR = ()
+WQSQ_FIRST = 8
 
 FLOPS = 2 * B * NX * NH + 2 * B * NH * NY
 
@@ -57,6 +60,8 @@ def tile_tnet_kernel(tc, x, W_fc_words, W_fc_scales, b_fc, W_q, out):
 
         for rt in range(X_FIRST):
             load_x(rt)
+        zeros = keep.tile([P, 512], BF16)
+        nc.vector.memset(zeros[:], 0.0)
         w_planes = keep.tile([P, N_PASS, NH], U8, align_bytes=64)
         nc.vector.memset(w_planes[:].bitcast(I32), 0)
         bias_rows = keep.tile([P, P], BF16)
@@ -89,12 +94,21 @@ def tile_tnet_kernel(tc, x, W_fc_words, W_fc_scales, b_fc, W_q, out):
             nc.tensor.transpose(bias_ps[:], bias_rows[:], ident_bf16[:])
             nc.vector.tensor_copy(out=bias[:], in_=bias_ps[:, 0:N_HID])
 
+        def keep_warm(n):
+            if n:
+                unread = psum.tile([P, 512], F32, tag="bank", bufs=8)
+                for _ in range(n):
+                    nc.tensor.matmul(out=unread[:], lhsT=zeros[:, 0:P], rhs=zeros[:], start=True, stop=True)
+
         ww_col = keep.tile([P, NY // P], F32)
         wq_grouped = keep.tile([P, NY, 4], BF16, align_bytes=64)
         wq_codes = keep.tile([P, NY], U32, align_bytes=64)
         wq_scales = keep.tile([P, NY], U8, align_bytes=64)
         ww_half = keep.tile([P, NY], F32)
 
+        shifts = keep.tile([P, NEWTON], F32)
+        for k in range(NEWTON):
+            nc.vector.memset(shifts[:, k : k + 1], float(k - NEWTON))
         one = keep.tile([P, 1], F32)
         nc.vector.memset(one[:], 1.0)
         zero = keep.tile([P, 1], F32)
@@ -301,18 +315,15 @@ def tile_tnet_kernel(tc, x, W_fc_words, W_fc_scales, b_fc, W_q, out):
                 out=weights[:], in_=state["q", rt][:], func=ACT.Exp, scale=-1.0, accum_out=column
             )
 
-        def guess_of_log(rnd_sums, y):
+        def guess_of_log(total, u):
             nc.vector.tensor_scalar(
-                out=y, in0=rnd_sums.bitcast(I32), scalar1=LN2 / 2.0**23, scalar2=(0.043 - 127.0) * LN2,
+                out=u, in0=total.bitcast(I32), scalar1=LN2 / 2.0**23, scalar2=(0.043 - 127.0) * LN2 - NEWTON,
                 op0=ALU.mult, op1=ALU.add,
             )
 
-        def newton_exp(y, e):
-            nc.scalar.activation(out=e, in_=y, func=ACT.Exp, scale=-1.0)
-
-        def newton_update(rnd_sums, y, e):
-            nc.vector.tensor_tensor(out=e, in0=e, in1=rnd_sums, op=ALU.mult)
-            nc.vector.scalar_tensor_tensor(out=y, in0=e, scalar=-1.0, in1=y, op0=ALU.add, op1=ALU.add)
+        def newton_step(total, u, e, k):
+            nc.scalar.activation(out=e, in_=u, func=ACT.Exp, scale=-1.0, bias=shifts[:, k : k + 1])
+            nc.vector.scalar_tensor_tensor(out=u, in0=e, scalar=total, in1=u, op0=ALU.mult, op1=ALU.add)
 
         def finish(rt, lse):
             q = state["q", rt]
@@ -327,31 +338,25 @@ def tile_tnet_kernel(tc, x, W_fc_words, W_fc_scales, b_fc, W_q, out):
         for group in GROUPS:
             steps_of_scalar += [("log", rt, group) for rt in group]
             steps_of_scalar += [("exp", rt, group) for rt in group]
-            if group != GROUPS[-1] or not NEWTON:
+            if group != GROUPS[-1]:
                 steps_of_scalar.append(("sum", group[-1], group))
         unfinished = []
-        small = []
+        streaming = []
 
-        def start_lse(sums, tiles):
-            n = len(tiles)
-            y = work.tile([P, n], F32, tag="y" + str(n), bufs=4)
-            e = work.tile([P, n], F32, tag="e" + str(n), bufs=4)
-            small.append(lambda: guess_of_log(sums, y[:]))
-            for _ in range(ITS):
-                small.append(lambda: newton_exp(y[:], e[:]))
-                small.append(lambda: newton_update(sums, y[:], e[:]))
-            small.append(lambda: unfinished.extend((rt, y[:, i : i + 1]) for i, rt in enumerate(tiles)))
-
-        def little(n=1):
-            for piece in small[:n]:
-                piece()
-            for piece in small[:n]:
-                small.remove(piece)
+        def stream():
+            for item in list(streaming):
+                rt, total, u, e, k = item
+                if k < NEWTON:
+                    newton_step(total, u, e, k)
+                    item[4] = k + 1
+                else:
+                    streaming.remove(item)
+                    finish(rt, u)
 
         def advance(n, newest):
             while n > 0 and steps_of_scalar:
                 kind, rt, group = steps_of_scalar[0]
-                nxt = steps_of_scalar[1][1] if kind == "sum" and len(steps_of_scalar) > 1 else rt
+                nxt = steps_of_scalar[1][1] if kind == "sum" else rt
                 if kind != "exp" and round_of[nxt] > newest:
                     return
                 steps_of_scalar.pop(0)
@@ -366,11 +371,14 @@ def tile_tnet_kernel(tc, x, W_fc_words, W_fc_scales, b_fc, W_q, out):
                     if i == 0:
                         sums = work.tile([P, len(group)], F32, tag="sums" + str(len(group)))
                         state["sums", group] = sums
-                    exp_tile(rt, state["sums", group][:, i : i + 1])
-                    if NEWTON and group == GROUPS[-1] and ((i + 1) % PER == 0 or i == len(group) - 1):
-                        j = i // PER * PER
-                        start_lse(state["sums", group][:, j : i + 1], group[j : i + 1])
-                little()
+                    column = state["sums", group][:, i : i + 1]
+                    exp_tile(rt, column)
+                    if group == GROUPS[-1]:
+                        stream()
+                        u = work.tile([P, 1], F32, tag="u", bufs=4)
+                        e = work.tile([P, 1], F32, tag="e", bufs=4)
+                        guess_of_log(column, u[:])
+                        streaming.append([rt, column, u[:], e[:], 0])
                 n -= 1
 
         def finish_some(n):
@@ -379,6 +387,7 @@ def tile_tnet_kernel(tc, x, W_fc_words, W_fc_scales, b_fc, W_q, out):
             for done in unfinished[:n]:
                 unfinished.remove(done)
 
+        keep_warm(WARM_0)
         norms_of_wq(0, WQSQ_FIRST)
         for step in range(n_rounds + 2):
             r0, r1, r2 = step, step - 1, step - 2
@@ -409,20 +418,21 @@ def tile_tnet_kernel(tc, x, W_fc_words, W_fc_scales, b_fc, W_q, out):
                 relu_x(r0, 1)
             if middle:
                 quantise_h(r1)
+                keep_warm(WARM_3)
                 products(r1)
+                keep_warm(WARM_4)
             if front:
                 quantise_a(r0)
             if step == 0:
                 spread_bias()
+                keep_warm(WARM_1)
                 for pair in range(4):
                     transpose_wq(pair)
+                    keep_warm(WARM_2)
                 quantise_wq()
             finish_some(FIN)
             advance(SLOT_B, r2)
-        while steps_of_scalar:
-            advance(1, n_rounds)
-            little()
-            finish_some(2)
-        while small or unfinished:
-            little()
-            finish_some(2)
+        finish_some(N_TILE)
+        advance(2 * N_TILE, n_rounds)
+        while streaming:
+            stream()

@@ -31,6 +31,9 @@ X_FIRST = 1
 SLOT_A = 2
 SLOT_B = 3
 NEWTON = 3
+HT_FIRST = False
+X_PIECES = 2
+WQ_PIECES = 2
 FIN = 3
 WARM_0 = 0
 WARM_1 = 0
@@ -55,7 +58,10 @@ def tile_tnet_kernel(tc, x, W_fc_words, W_fc_scales, b_fc, W_q, out):
 
         def load_x(rt):
             x_rt = work.tile([P, NX], BF16, tag="x_rt", bufs=16)
-            nc.sync.dma_start(out=x_rt[:], in_=x[rt * P : (rt + 1) * P, :])
+            pieces = X_PIECES if rt == 0 else 1
+            for piece in range(pieces):
+                cols = slice(piece * NX // pieces, (piece + 1) * NX // pieces)
+                nc.sync.dma_start(out=x_rt[:, cols], in_=x[rt * P : (rt + 1) * P, cols])
             x_tiles.append(x_rt)
 
         for rt in range(X_FIRST):
@@ -73,7 +79,9 @@ def tile_tnet_kernel(tc, x, W_fc_words, W_fc_scales, b_fc, W_q, out):
             )
         nc.sync.dma_start(out=bias_rows[0:N_HID, :], in_=b_fc.rearrange("(c p) -> c p", p=P))
         wq_rows = keep.tile([P, NY // P, NH], BF16)
-        nc.sync.dma_start(out=wq_rows[:], in_=W_q.rearrange("(a p) k -> p a k", p=P))
+        for piece in range(WQ_PIECES):
+            rows = slice(piece * NY // P // WQ_PIECES, (piece + 1) * NY // P // WQ_PIECES)
+            nc.sync.dma_start(out=wq_rows[:, rows, :], in_=W_q.rearrange("(a p) k -> p a k", p=P)[:, rows, :])
         w_codes = keep.tile([P, N_PASS, NH], U32, align_bytes=64)
         nc.sync.dma_start(
             out=w_codes[:].bitcast(I32),
@@ -161,12 +169,14 @@ def tile_tnet_kernel(tc, x, W_fc_words, W_fc_scales, b_fc, W_q, out):
             x_words = x_tiles[ROUNDS[rnd][t]][:].bitcast(F32)
             banks = []
             for pair in range(N_PASS // 2):
-                xt = psum.tile([P, 2, P, 2], F32, tag="bank", bufs=8)
+                on_scalar = t == 0 and rnd in RELU_ON_SCALAR
+                xt = psum.tile([P, 2, 2, P] if on_scalar else [P, 2, P, 2], F32, tag="bank", bufs=8)
+                planes = xt[:].rearrange("p u g i -> p g i u") if on_scalar else xt[:]
                 for gi in range(2):
                     g = 2 * pair + gi
                     for u in range(2):
                         nc.tensor.transpose(
-                            xt[:, gi, :, u], x_words[:, 256 * g + u : 256 * (g + 1) : 2], ident_f32[:]
+                            planes[:, gi, :, u], x_words[:, 256 * g + u : 256 * (g + 1) : 2], ident_f32[:]
                         )
                 banks.append(xt)
             state["xt", rnd, t] = banks
@@ -178,6 +188,9 @@ def tile_tnet_kernel(tc, x, W_fc_words, W_fc_scales, b_fc, W_q, out):
             for pair in range(N_PASS // 2):
                 grouped = state["a_grouped", rnd][:, 2 * pair : 2 * pair + 2, t * P : (t + 1) * P, :]
                 bank = state["xt", rnd, t][pair][:].bitcast(BF16)
+                if t == 0 and rnd in RELU_ON_SCALAR:
+                    bank = bank.rearrange("p u g (i e) -> p g i u e", e=2)
+                    grouped = grouped.rearrange("p g i (u e) -> p g i u e", e=2)
                 if t == 0 and rnd in RELU_ON_SCALAR:
                     nc.scalar.activation(out=grouped, in_=bank, func=ACT.Relu)
                 else:
@@ -395,8 +408,9 @@ def tile_tnet_kernel(tc, x, W_fc_words, W_fc_scales, b_fc, W_q, out):
             if middle:
                 hidden_product(r1)
             if front:
-                for t in range(len(ROUNDS[r0])):
-                    transpose_x(r0, t)
+                transpose_x(r0, 0)
+                if not HT_FIRST and len(ROUNDS[r0]) > 1:
+                    transpose_x(r0, 1)
             if middle and r1 not in HIDDEN_ON_VECTOR:
                 hidden_layer(r1)
             if step == 1:
@@ -413,6 +427,9 @@ def tile_tnet_kernel(tc, x, W_fc_words, W_fc_scales, b_fc, W_q, out):
             if middle:
                 transpose_h(r1)
                 norms_of_h(r1)
+            if HT_FIRST and front and len(ROUNDS[r0]) > 1:
+                transpose_x(r0, 1)
+            if middle:
                 round_h(r1)
             if front and len(ROUNDS[r0]) > 1:
                 relu_x(r0, 1)

@@ -25,15 +25,18 @@ ROOT_HALF = 0.5**0.5
 LN2 = math.log(2.0)
 
 GROUPS = ((0, 1, 2, 3, 4, 5, 6, 7, 8,), (9, 10, 11, 12, 13, 14, 15,))
-RELU_ON_SCALAR = tuple(range(2, 7))
+RELU_ON_SCALAR = tuple(range(1, 7))
 HIDDEN_ON_VECTOR = (6, 7, 8)
 X_FIRST = 1
-SLOT_A = 2
-SLOT_B = 3
+SLOT_A = 3
+SLOT_B = 2
 NEWTON = 3
 HT_FIRST = False
 X_PIECES = 2
 WQ_PIECES = 2
+LAST_PIECES = 2
+PREFETCH = ()
+WW_AT = 2
 FIN = 3
 WARM_0 = 0
 WARM_1 = 0
@@ -154,12 +157,10 @@ def tile_tnet_kernel(tc, x, W_fc_words, W_fc_scales, b_fc, W_q, out):
             for half in range(N_HALF):
                 ww_ps = psum.tile([P, 512], F32, tag="bank", bufs=8)
                 for a in range(4):
-                    nc.tensor.matmul(
-                        out=ww_ps[:, a * P : (a + 1) * P],
-                        lhsT=ww_col[:, 4 * half + a : 4 * half + a + 1].to_broadcast([P, P]),
-                        rhs=ident_f32[:],
-                        start=True,
-                        stop=True,
+                    nc.tensor.transpose(
+                        ww_ps[:, a * P : (a + 1) * P],
+                        ww_col[:, 4 * half + a : 4 * half + a + 1].to_broadcast([P, P]),
+                        ident_f32[:],
                     )
                 nc.scalar.copy(out=ww_half[:, 512 * half : 512 * (half + 1)], in_=ww_ps[:])
 
@@ -340,10 +341,13 @@ def tile_tnet_kernel(tc, x, W_fc_words, W_fc_scales, b_fc, W_q, out):
 
         def finish(rt, lse):
             q = state["q", rt]
-            nc.vector.tensor_scalar(
-                out=q[:], in0=q[:], scalar1=-1.0, scalar2=lse, op0=ALU.mult, op1=ALU.subtract
-            )
-            nc.sync.dma_start(out=out[rt * P : (rt + 1) * P, :], in_=q[:])
+            pieces = LAST_PIECES if rt == N_TILE - 1 else 1
+            for piece in range(pieces):
+                cols = slice(piece * NY // pieces, (piece + 1) * NY // pieces)
+                nc.vector.tensor_scalar(
+                    out=q[:, cols], in0=q[:, cols], scalar1=-1.0, scalar2=lse, op0=ALU.mult, op1=ALU.subtract
+                )
+                nc.sync.dma_start(out=out[rt * P : (rt + 1) * P, cols], in_=q[:, cols])
 
         n_rounds = len(ROUNDS)
         round_of = {rt: rnd for rnd, tiles in enumerate(ROUNDS) for rt in tiles}
@@ -407,14 +411,13 @@ def tile_tnet_kernel(tc, x, W_fc_words, W_fc_scales, b_fc, W_q, out):
             front, middle, back = r0 < n_rounds, 0 <= r1 < n_rounds, 0 <= r2 < n_rounds
             if middle:
                 hidden_product(r1)
-            if front:
+            if front and r0 not in PREFETCH:
                 transpose_x(r0, 0)
-                if not HT_FIRST and len(ROUNDS[r0]) > 1:
+                if len(ROUNDS[r0]) > 1:
                     transpose_x(r0, 1)
             if middle and r1 not in HIDDEN_ON_VECTOR:
                 hidden_layer(r1)
-            if step == 1:
-                norms_of_wq(WQSQ_FIRST, 8)
+            if step == 1 and WW_AT == 1:
                 spread_norms_of_wq()
             if back:
                 distances(r2)
@@ -427,12 +430,15 @@ def tile_tnet_kernel(tc, x, W_fc_words, W_fc_scales, b_fc, W_q, out):
             if middle:
                 transpose_h(r1)
                 norms_of_h(r1)
-            if HT_FIRST and front and len(ROUNDS[r0]) > 1:
-                transpose_x(r0, 1)
             if middle:
                 round_h(r1)
             if front and len(ROUNDS[r0]) > 1:
                 relu_x(r0, 1)
+            if step == 1 and WW_AT == 2:
+                spread_norms_of_wq()
+            if step + 1 in PREFETCH:
+                transpose_x(step + 1, 0)
+                transpose_x(step + 1, 1)
             if middle:
                 quantise_h(r1)
                 keep_warm(WARM_3)

@@ -335,9 +335,12 @@ def tile_tnet_kernel(tc, x, W_fc_words, W_fc_scales, b_fc, W_q, out):
                 op0=ALU.mult, op1=ALU.add,
             )
 
-        def newton_step(total, u, e, k):
+        def newton_step(total, u, e, k, on_scalar):
             nc.scalar.activation(out=e, in_=u, func=ACT.Exp, scale=-1.0, bias=shifts[:, k : k + 1])
-            nc.vector.scalar_tensor_tensor(out=u, in0=e, scalar=total, in1=u, op0=ALU.mult, op1=ALU.add)
+            if on_scalar:
+                nc.scalar.activation(out=u, in_=e, func=ACT.Identity, scale=total, bias=u)
+            else:
+                nc.vector.scalar_tensor_tensor(out=u, in0=e, scalar=total, in1=u, op0=ALU.mult, op1=ALU.add)
 
         def finish(rt, lse):
             q = state["q", rt]
@@ -364,7 +367,7 @@ def tile_tnet_kernel(tc, x, W_fc_words, W_fc_scales, b_fc, W_q, out):
             for item in list(streaming):
                 rt, total, u, e, k = item
                 if k < NEWTON:
-                    newton_step(total, u, e, k)
+                    newton_step(total, u, e, k, rt == N_TILE - 1)
                     item[4] = k + 1
                 else:
                     streaming.remove(item)
@@ -453,7 +456,7 @@ def tile_tnet_kernel(tc, x, W_fc_words, W_fc_scales, b_fc, W_q, out):
                     transpose_wq(pair)
                     keep_warm(WARM_2)
                 quantise_wq()
-            finish_some(FIN)
+            finish_some(FIN if step <= n_rounds else N_TILE)
             advance(SLOT_B, r2)
         finish_some(N_TILE)
         advance(2 * N_TILE, n_rounds)

import math
from contextlib import ExitStack

import concourse.mybir as mybir
from concourse.masks import make_identity

F32 = mybir.dt.float32
BF16 = mybir.dt.bfloat16
I32 = mybir.dt.int32
U32 = mybir.dt.uint32
U8 = mybir.dt.uint8
FP8X4 = mybir.dt.float8_e4m3fn_x4
ACT = mybir.ActivationFunctionType
ALU = mybir.AluOpType

P = 128
B, NX, NH, NY = 2048, 2048, 512, 1024
K_PASS = 4 * P
N_PASS = NX // K_PASS
N_HID = NH // P
N_TILE = B // P
ROUNDS = ((0,),) + tuple((i, i + 1) for i in range(1, N_TILE - 2, 2)) + ((N_TILE - 1,),)
N_HALF = NY // 512
ROOT_HALF = 0.5**0.5
LN2 = math.log(2.0)

GROUPS = ((0, 1, 2, 3, 4, 5, 6, 7, 8,), (9, 10, 11, 12, 13, 14, 15,))
RELU_ON_SCALAR = tuple(range(1, 7))
HIDDEN_ON_VECTOR = (6, 7, 8)
X_FIRST = 1
SLOT_A = 3
SLOT_B = 2
NEWTON = 3
HT_FIRST = False
X_PIECES = 2
WQ_PIECES = 2
LAST_PIECES = 2
PREFETCH = ()
WW_AT = 2
FIN = 3
WARM_0 = 0
WARM_1 = 0
WARM_2 = 0
WARM_3 = 0
WARM_4 = 0
WQ_ON_SCALAR = ()
WQSQ_FIRST = 8

FLOPS = 2 * B * NX * NH + 2 * B * NH * NY


def tile_tnet_kernel(tc, x, W_fc_words, W_fc_scales, b_fc, W_q, out):
    nc = tc.nc
    with ExitStack() as ctx:
        keep = ctx.enter_context(tc.tile_pool(name="keep", bufs=1))
        work = ctx.enter_context(tc.tile_pool(name="work", bufs=2))
        psum = ctx.enter_context(tc.psum_pool(name="psum", bufs=1))
        ctx.enter_context(tc.manual_schedule())

        x_tiles = []

        def load_x(rt):
            x_rt = work.tile([P, NX], BF16, tag="x_rt", bufs=16)
            pieces = X_PIECES if rt == 0 else 1
            for piece in range(pieces):
                cols = slice(piece * NX // pieces, (piece + 1) * NX // pieces)
                nc.sync.dma_start(out=x_rt[:, cols], in_=x[rt * P : (rt + 1) * P, cols])
            x_tiles.append(x_rt)

        for rt in range(X_FIRST):
            load_x(rt)
        zeros = keep.tile([P, 512], BF16)
        nc.vector.memset(zeros[:], 0.0)
        w_planes = keep.tile([P, N_PASS, NH], U8, align_bytes=64)
        nc.vector.memset(w_planes[:].bitcast(I32), 0)
        bias_rows = keep.tile([P, P], BF16)
        nc.vector.memset(bias_rows[:], 0.0)
        for quad in range(4):
            nc.sync.dma_start(
                out=w_planes[32 * quad : 32 * quad + 4, :, :].bitcast(I32),
                in_=W_fc_scales[:, 4 * quad : 4 * quad + 4, :].rearrange("g r n -> r g n").bitcast(I32),
            )
        nc.sync.dma_start(out=bias_rows[0:N_HID, :], in_=b_fc.rearrange("(c p) -> c p", p=P))
        wq_rows = keep.tile([P, NY // P, NH], BF16)
        for piece in range(WQ_PIECES):
            rows = slice(piece * NY // P // WQ_PIECES, (piece + 1) * NY // P // WQ_PIECES)
            nc.sync.dma_start(out=wq_rows[:, rows, :], in_=W_q.rearrange("(a p) k -> p a k", p=P)[:, rows, :])
        w_codes = keep.tile([P, N_PASS, NH], U32, align_bytes=64)
        nc.sync.dma_start(
            out=w_codes[:].bitcast(I32),
            in_=W_fc_words.rearrange("g p n t -> p g (n t)").bitcast(I32),
        )
        for rt in range(len(x_tiles), N_TILE):
            load_x(rt)

        ident_f32 = keep.tile([P, P], F32)
        make_identity(nc, ident_f32[:])
        ident_bf16 = keep.tile([P, P], BF16)
        make_identity(nc, ident_bf16[:])

        bias = keep.tile([P, N_HID], F32)

        def spread_bias():
            bias_ps = psum.tile([P, P], BF16, tag="bank", bufs=8)
            nc.tensor.transpose(bias_ps[:], bias_rows[:], ident_bf16[:])
            nc.vector.tensor_copy(out=bias[:], in_=bias_ps[:, 0:N_HID])

        def keep_warm(n):
            if n:
                unread = psum.tile([P, 512], F32, tag="bank", bufs=8)
                for _ in range(n):
                    nc.tensor.matmul(out=unread[:], lhsT=zeros[:, 0:P], rhs=zeros[:], start=True, stop=True)

        ww_col = keep.tile([P, NY // P], F32)
        wq_grouped = keep.tile([P, NY, 4], BF16, align_bytes=64)
        wq_codes = keep.tile([P, NY], U32, align_bytes=64)
        wq_scales = keep.tile([P, NY], U8, align_bytes=64)
        ww_half = keep.tile([P, NY], F32)

        shifts = keep.tile([P, NEWTON], F32)
        for k in range(NEWTON):
            nc.vector.memset(shifts[:, k : k + 1], float(k - NEWTON))
        one = keep.tile([P, 1], F32)
        nc.vector.memset(one[:], 1.0)
        zero = keep.tile([P, 1], F32)
        nc.scalar.activation(out=zero[:], in_=one[:], func=ACT.Ln)

        def norms_of_wq(first, last):
            for a in range(first, last):
                squares = work.tile([P, NH], F32, tag="squares")
                nc.scalar.activation(
                    out=squares[:], in_=wq_rows[:, a, :], func=ACT.Square, scale=ROOT_HALF,
                    accum_out=ww_col[:, a : a + 1],
                )

        def transpose_wq(pair):
            wq_ps = psum.tile([P, 2, 4, P], BF16, tag="bank", bufs=8)
            for a in range(2):
                for t in range(4):
                    nc.tensor.transpose(
                        wq_ps[:, a, t, :], wq_rows[:, 2 * pair + a, t * P : (t + 1) * P], ident_bf16[:]
                    )
            grouped = wq_grouped[:, 2 * pair * P : (2 * pair + 2) * P, :].rearrange("p (a j) t -> p a j t", a=2)
            if pair in WQ_ON_SCALAR:
                nc.scalar.copy(out=grouped, in_=wq_ps[:].rearrange("p a t j -> p a j t"))
            else:
                nc.vector.tensor_copy(out=grouped, in_=wq_ps[:].rearrange("p a t j -> p a j t"))

        def quantise_wq():
            nc.vector.quantize_mx(
                out=wq_codes[:].bitcast(FP8X4),
                scales=wq_scales[:],
                in_=wq_grouped[:].rearrange("p j t -> p (j t)"),
            )

        def spread_norms_of_wq():
            for half in range(N_HALF):
                ww_ps = psum.tile([P, 512], F32, tag="bank", bufs=8)
                for a in range(4):
                    nc.tensor.transpose(
                        ww_ps[:, a * P : (a + 1) * P],
                        ww_col[:, 4 * half + a : 4 * half + a + 1].to_broadcast([P, P]),
                        ident_f32[:],
                    )
                nc.scalar.copy(out=ww_half[:, 512 * half : 512 * (half + 1)], in_=ww_ps[:])

        state = {}

        def transpose_x(rnd, t):
            x_words = x_tiles[ROUNDS[rnd][t]][:].bitcast(F32)
            banks = []
            for pair in range(N_PASS // 2):
                on_scalar = t == 0 and rnd in RELU_ON_SCALAR
                xt = psum.tile([P, 2, 2, P] if on_scalar else [P, 2, P, 2], F32, tag="bank", bufs=8)
                planes = xt[:].rearrange("p u g i -> p g i u") if on_scalar else xt[:]
                for gi in range(2):
                    g = 2 * pair + gi
                    for u in range(2):
                        nc.tensor.transpose(
                            planes[:, gi, :, u], x_words[:, 256 * g + u : 256 * (g + 1) : 2], ident_f32[:]
                        )
                banks.append(xt)
            state["xt", rnd, t] = banks

        def relu_x(rnd, t):
            if t == 0:
                a_grouped = work.tile([P, N_PASS, len(ROUNDS[rnd]) * P, 4], BF16, tag="a_grouped", align_bytes=64)
                state["a_grouped", rnd] = a_grouped
            for pair in range(N_PASS // 2):
                grouped = state["a_grouped", rnd][:, 2 * pair : 2 * pair + 2, t * P : (t + 1) * P, :]
                bank = state["xt", rnd, t][pair][:].bitcast(BF16)
                if t == 0 and rnd in RELU_ON_SCALAR:
                    bank = bank.rearrange("p u g (i e) -> p g i u e", e=2)
                    grouped = grouped.rearrange("p g i (u e) -> p g i u e", e=2)
                if t == 0 and rnd in RELU_ON_SCALAR:
                    nc.scalar.activation(out=grouped, in_=bank, func=ACT.Relu)
                else:
                    nc.vector.tensor_scalar_max(out=grouped, in0=bank, scalar1=0.0)

        def quantise_a(rnd):
            n = len(ROUNDS[rnd]) * P
            a_codes = work.tile([P, N_PASS, n], U32, tag="a_codes", align_bytes=64)
            a_scales = work.tile([P, N_PASS, n], U8, tag="a_scales", align_bytes=64)
            nc.vector.quantize_mx(
                out=a_codes[:].rearrange("p g b -> p (g b)").bitcast(FP8X4),
                scales=a_scales[:].rearrange("p g b -> p (g b)"),
                in_=state["a_grouped", rnd][:].rearrange("p g b t -> p (g b t)"),
            )
            state["a", rnd] = (a_codes, a_scales)

        def hidden_product(rnd):
            n = len(ROUNDS[rnd]) * P
            a_codes, a_scales = state["a", rnd]
            per_bank = 512 // n
            accs = []
            for c in range(N_HID):
                if c % per_bank == 0:
                    acc1 = psum.tile([P, per_bank, n], F32, tag="bank", bufs=8)
                for g in range(N_PASS):
                    nc.tensor.matmul_mx(
                        out=acc1[:, c % per_bank, :],
                        lhsT=w_codes[:, g, c * P : (c + 1) * P].bitcast(FP8X4),
                        lhsT_scale=w_planes[:, g, c * P : (c + 1) * P],
                        rhs=a_codes[:, g, :].bitcast(FP8X4),
                        rhs_scale=a_scales[:, g, :],
                        start=(g == 0),
                        stop=(g == N_PASS - 1),
                    )
                accs.append(acc1[:, c % per_bank, :])
            state["acc1", rnd] = accs

        def hidden_layer(rnd):
            h_f32 = work.tile([P, N_HID, len(ROUNDS[rnd]) * P], F32, tag="h_f32", bufs=3)
            for c in range(N_HID):
                if rnd in HIDDEN_ON_VECTOR:
                    nc.vector.tensor_scalar(
                        out=h_f32[:, c, :], in0=state["acc1", rnd][c], scalar1=bias[:, c : c + 1], scalar2=0.0,
                        op0=ALU.add, op1=ALU.max,
                    )
                else:
                    nc.scalar.activation(
                        out=h_f32[:, c, :], in_=state["acc1", rnd][c], func=ACT.Relu, bias=bias[:, c : c + 1]
                    )
            state["h", rnd] = h_f32

        def round_h(rnd):
            h_grouped = work.tile([P, len(ROUNDS[rnd]) * P, 4], BF16, tag="h_grouped", align_bytes=64)
            nc.vector.tensor_copy(out=h_grouped[:], in_=state["h", rnd][:].rearrange("p c b -> p b c"))
            state["h_grouped", rnd] = h_grouped

        def quantise_h(rnd):
            n = len(ROUNDS[rnd]) * P
            h_codes = work.tile([P, n], U32, tag="h_codes", align_bytes=64)
            h_scales = work.tile([P, n], U8, tag="h_scales", align_bytes=64)
            nc.vector.quantize_mx(
                out=h_codes[:].bitcast(FP8X4),
                scales=h_scales[:],
                in_=state["h_grouped", rnd][:].rearrange("p b c -> p (b c)"),
            )
            state["hq", rnd] = (h_codes, h_scales)

        def transpose_h(rnd):
            h_f32 = state["h", rnd]
            banks = []
            for t in range(len(ROUNDS[rnd])):
                h_rows = psum.tile([P, N_HID, P], F32, tag="bank", bufs=8)
                for k in range(N_HID):
                    nc.tensor.transpose(h_rows[:, k, :], h_f32[:, k, t * P : (t + 1) * P], ident_f32[:])
                banks.append(h_rows)
            state["h_rows", rnd] = banks

        def norms_of_h(rnd):
            hh = work.tile([P, 2], F32, tag="hh", bufs=3)
            for t in range(len(ROUNDS[rnd])):
                squares = work.tile([P, NH], F32, tag="squares")
                nc.scalar.activation(
                    out=squares[:],
                    in_=state["h_rows", rnd][t][:].rearrange("p k n -> p (k n)"),
                    func=ACT.Square,
                    scale=ROOT_HALF,
                    accum_out=hh[:, t : t + 1],
                )
            state["hh", rnd] = hh

        def products(rnd):
            h_codes, h_scales = state["hq", rnd]
            for t in range(len(ROUNDS[rnd])):
                for half in range(N_HALF):
                    cols = slice(512 * half, 512 * (half + 1))
                    acc2 = psum.tile([P, 512], F32, tag="bank", bufs=8)
                    nc.tensor.matmul_mx(
                        out=acc2[:],
                        lhsT=h_codes[:, t * P : (t + 1) * P].bitcast(FP8X4),
                        lhsT_scale=h_scales[:, t * P : (t + 1) * P],
                        rhs=wq_codes[:, cols].bitcast(FP8X4),
                        rhs_scale=wq_scales[:, cols],
                        start=True,
                        stop=True,
                    )
                    state["acc2", rnd, t, half] = acc2

        def distances(rnd):
            for t, rt in enumerate(ROUNDS[rnd]):
                q = work.tile([P, NY], F32, tag="q", bufs=16)
                for half in range(N_HALF):
                    cols = slice(512 * half, 512 * (half + 1))
                    nc.vector.scalar_tensor_tensor(
                        out=q[:, cols],
                        in0=state["acc2", rnd, t, half][:],
                        scalar=state["hh", rnd][:, t : t + 1],
                        in1=ww_half[:, cols],
                        op0=ALU.subtract,
                        op1=ALU.subtract,
                    )
                state["q", rt] = q

        def clamp(rnd):
            for rt in ROUNDS[rnd]:
                q = state["q", rt]
                nc.vector.tensor_scalar_min(out=q[:], in0=q[:], scalar1=0.0)

        def log_tile(rt):
            q = state["q", rt]
            nc.scalar.activation(out=q[:], in_=q[:], func=ACT.Ln, scale=-2.0, bias=one[:])

        def exp_tile(rt, column):
            weights = work.tile([P, NY], F32, tag="weights")
            nc.scalar.activation(
                out=weights[:], in_=state["q", rt][:], func=ACT.Exp, scale=-1.0, accum_out=column
            )

        def guess_of_log(total, u):
            nc.vector.tensor_scalar(
                out=u, in0=total.bitcast(I32), scalar1=LN2 / 2.0**23, scalar2=(0.043 - 127.0) * LN2 - NEWTON,
                op0=ALU.mult, op1=ALU.add,
            )

        def newton_step(total, u, e, k, on_scalar):
            nc.scalar.activation(out=e, in_=u, func=ACT.Exp, scale=-1.0, bias=shifts[:, k : k + 1])
            if on_scalar:
                nc.scalar.activation(out=u, in_=e, func=ACT.Identity, scale=total, bias=u)
            else:
                nc.vector.scalar_tensor_tensor(out=u, in0=e, scalar=total, in1=u, op0=ALU.mult, op1=ALU.add)

        def finish(rt, lse):
            q = state["q", rt]
            pieces = LAST_PIECES if rt == N_TILE - 1 else 1
            for piece in range(pieces):
                cols = slice(piece * NY // pieces, (piece + 1) * NY // pieces)
                nc.vector.tensor_scalar(
                    out=q[:, cols], in0=q[:, cols], scalar1=-1.0, scalar2=lse, op0=ALU.mult, op1=ALU.subtract
                )
                nc.sync.dma_start(out=out[rt * P : (rt + 1) * P, cols], in_=q[:, cols])

        n_rounds = len(ROUNDS)
        round_of = {rt: rnd for rnd, tiles in enumerate(ROUNDS) for rt in tiles}
        steps_of_scalar = []
        for group in GROUPS:
            steps_of_scalar += [("log", rt, group) for rt in group]
            steps_of_scalar += [("exp", rt, group) for rt in group]
            if group != GROUPS[-1]:
                steps_of_scalar.append(("sum", group[-1], group))
        unfinished = []
        streaming = []

        def stream():
            for item in list(streaming):
                rt, total, u, e, k = item
                if k < NEWTON:
                    newton_step(total, u, e, k, rt == N_TILE - 1)
                    item[4] = k + 1
                else:
                    streaming.remove(item)
                    finish(rt, u)

        def advance(n, newest):
            while n > 0 and steps_of_scalar:
                kind, rt, group = steps_of_scalar[0]
                nxt = steps_of_scalar[1][1] if kind == "sum" else rt
                if kind != "exp" and round_of[nxt] > newest:
                    return
                steps_of_scalar.pop(0)
                i = group.index(rt)
                if kind == "sum":
                    lse = work.tile([P, len(group)], F32, tag="lse" + str(len(group)))
                    nc.scalar.activation(out=lse[:], in_=state["sums", group][:], func=ACT.Ln)
                    unfinished.extend((rt2, lse[:, i2 : i2 + 1]) for i2, rt2 in enumerate(group))
                elif kind == "log":
                    log_tile(rt)
                else:
                    if i == 0:
                        sums = work.tile([P, len(group)], F32, tag="sums" + str(len(group)))
                        state["sums", group] = sums
                    column = state["sums", group][:, i : i + 1]
                    exp_tile(rt, column)
                    if group == GROUPS[-1]:
                        stream()
                        u = work.tile([P, 1], F32, tag="u", bufs=4)
                        e = work.tile([P, 1], F32, tag="e", bufs=4)
                        guess_of_log(column, u[:])
                        streaming.append([rt, column, u[:], e[:], 0])
                n -= 1

        def finish_some(n):
            for tile_and_lse in unfinished[:n]:
                finish(*tile_and_lse)
            for done in unfinished[:n]:
                unfinished.remove(done)

        keep_warm(WARM_0)
        norms_of_wq(0, WQSQ_FIRST)
        for step in range(n_rounds + 2):
            r0, r1, r2 = step, step - 1, step - 2
            front, middle, back = r0 < n_rounds, 0 <= r1 < n_rounds, 0 <= r2 < n_rounds
            if middle:
                hidden_product(r1)
            if front and r0 not in PREFETCH:
                transpose_x(r0, 0)
                if len(ROUNDS[r0]) > 1:
                    transpose_x(r0, 1)
            if middle and r1 not in HIDDEN_ON_VECTOR:
                hidden_layer(r1)
            if step == 1 and WW_AT == 1:
                spread_norms_of_wq()
            if back:
                distances(r2)
                clamp(r2)
            if middle and r1 in HIDDEN_ON_VECTOR:
                hidden_layer(r1)
            advance(SLOT_A, r2 - 1)
            if front:
                relu_x(r0, 0)
            if middle:
                transpose_h(r1)
                norms_of_h(r1)
            if middle:
                round_h(r1)
            if front and len(ROUNDS[r0]) > 1:
                relu_x(r0, 1)
            if step == 1 and WW_AT == 2:
                spread_norms_of_wq()
            if step + 1 in PREFETCH:
                transpose_x(step + 1, 0)
                transpose_x(step + 1, 1)
            if middle:
                quantise_h(r1)
                keep_warm(WARM_3)
                products(r1)
                keep_warm(WARM_4)
            if front:
                quantise_a(r0)
            if step == 0:
                spread_bias()
                keep_warm(WARM_1)
                for pair in range(4):
                    transpose_wq(pair)
                    keep_warm(WARM_2)
                quantise_wq()
            finish_some(FIN if step <= n_rounds else N_TILE)
            advance(SLOT_B, r2)
        finish_some(N_TILE)
        advance(2 * N_TILE, n_rounds)
        while streaming:
            stream()
